import numpy as np
import ml_dtypes


def mxq(x, axis, fmt="e4m3"):
    dtype, down = {"e4m3": (ml_dtypes.float8_e4m3fn, 7), "e5m2": (ml_dtypes.float8_e5m2, 14)}[fmt]
    v = np.moveaxis(np.asarray(x, np.float32).astype(ml_dtypes.bfloat16).astype(np.float64), axis, -1)
    blocks = v.reshape(v.shape[:-1] + (-1, 32))
    amax = np.abs(blocks).max(-1, keepdims=True)
    byte = np.maximum(np.where(amax > 0, np.frexp(amax)[1] - 1 + 127, 0) - down, 1)
    scale = np.exp2(byte - 127.0)
    codes = (blocks / scale).astype(np.float32).astype(dtype).astype(np.float64)
    return np.moveaxis((codes * scale).reshape(v.shape), -1, axis)


WIDE = False


def mx_kscale(k):
    if not WIDE:
        return np.ones(k)
    levels = np.array([20, -20, 10, -10, 0])
    a = np.random.permutation(np.resize(levels, k // 512 * 4)).reshape(k // 512, 4)
    idx = np.arange(k)
    return np.exp2(a[idx // 512, idx % 128 // 32])


BF16 = ml_dtypes.bfloat16


def bf(x):
    return np.asarray(x, np.float32).astype(BF16)


def f64(x):
    return np.asarray(x).astype(np.float64)


B, H = 1024, 1024


def sigmoid(v):
    return 1.0 / (1.0 + np.exp(-v))


def setup_inputs():
    s = mx_kscale(B)
    w = lambda: bf(np.random.standard_normal((H, H)) * 0.7 / np.sqrt(H))
    b = lambda: bf(np.random.standard_normal(H) * 0.5)
    x0 = bf(np.random.standard_normal((B, H)))
    h0 = bf(np.random.standard_normal((B, H)))
    Wf = w()
    b_f = b()
    Wi = w()
    b_i = b()
    Wg = w()
    b_g = b()
    Wo = w()
    b_o = b()
    g = bf(np.random.standard_normal((2, B, H)) * np.exp2(np.random.randint(-12, 1, (1, B, 1))) / s[None, :, None])
    z0 = f64(x0) + f64(h0)
    gate_f = sigmoid(z0 @ f64(Wf).T + f64(b_f))
    gate_o = sigmoid(z0 @ f64(Wo).T + f64(b_o))
    cell = gate_f + sigmoid(z0 @ f64(Wi).T + f64(b_i)) * np.tanh(z0 @ f64(Wg).T + f64(b_g))
    return {"inputs": bf(f64(x0) * s[:, None]),
            "short_term_memory": bf(f64(h0) * s[:, None]),
            "Wf": Wf, "b_f": b_f, "Wi": Wi, "b_i": b_i, "Wg": Wg, "b_g": b_g, "Wo": Wo, "b_o": b_o,
            "gate_f": np.asarray(gate_f, np.float32),
            "gate_o": np.asarray(gate_o, np.float32),
            "cell": np.asarray(cell, np.float32),
            "grad_out": g}


def reference(inputs, short_term_memory, Wf, b_f, Wi, b_i, Wg, b_g, Wo, b_o, gate_f, gate_o, cell, grad_out):
    g = f64(grad_out)
    z = f64(inputs) + f64(short_term_memory)
    f = f64(gate_f)
    o = f64(gate_o)
    tc = np.tanh(f64(cell))
    dc = g[0] + g[1] * o * (1.0 - tc * tc)
    da = dc * f * (1.0 - f)
    return mxq(da, 0, "e5m2").T @ mxq(z, 0, "e4m3")

@@ -1,0 +1,197 @@
+import concourse.mybir as mybir
+
+F32 = mybir.dt.float32
+BF16 = mybir.dt.bfloat16
+U32 = mybir.dt.uint32
+U8 = mybir.dt.uint8
+E4M3_X4 = mybir.dt.float8_e4m3fn_x4
+E5M2_X4 = mybir.dt.float8_e5m2_x4
+ACT = mybir.ActivationFunctionType
+ALU = mybir.AluOpType
+
+P = 128
+PACK = 4
+K_PASS = P * PACK
+TOKENS = 1024
+FEATURES = 1024
+PASSES = TOKENS // K_PASS
+HALF_ROWS = PACK // 2
+DA_COLS = 256
+Z_COLS = 512
+M_TILE = 128
+N_TILE = 512
+M_TILES = FEATURES // M_TILE
+N_TILES = FEATURES // N_TILE
+PSUM_BANKS = 8
+EARLY_M_TILES = PSUM_BANKS // N_TILES
+
+FLOPS = 2 * TOKENS * FEATURES * FEATURES
+BYTES = TOKENS * FEATURES * (2 + 2 + 4 + 4 + 4 + 2 + 2) + FEATURES * FEATURES * 4
+
+
+def tile_lstmcell_pa_v_kernel(
+    tc,
+    inputs,
+    short_term_memory,
+    Wf,
+    b_f,
+    Wi,
+    b_i,
+    Wg,
+    b_g,
+    Wo,
+    b_o,
+    gate_f,
+    gate_o,
+    cell,
+    grad_out,
+    out,
+):
+    nc = tc.nc
+    grad_rows = grad_out.flatten_outer_dims()
+    halves = [slice(u * HALF_ROWS, (u + 1) * HALF_ROWS) for u in range(PACK // HALF_ROWS)]
+
+    with (
+        tc.tile_pool(name="resident", bufs=1) as resident,
+        tc.tile_pool(name="grouped", bufs=3) as grouped,
+        tc.tile_pool(name="results", bufs=4) as results,
+        tc.psum_pool(name="psum", bufs=PSUM_BANKS) as psum,
+    ):
+        def pass_tiles(name, dtype):
+            return [
+                resident.tile([P, PACK, FEATURES], dtype, name="%s%d" % (name, c))
+                for c in range(PASSES)
+            ]
+
+        cell_t = pass_tiles("cell", F32)
+        o_t = pass_tiles("gate_o", F32)
+        f_t = pass_tiles("gate_f", F32)
+        gc_t = pass_tiles("grad_c", BF16)
+        gh_t = pass_tiles("grad_h", BF16)
+        x_t = pass_tiles("x", BF16)
+        h_t = pass_tiles("h", BF16)
+
+        da_codes = resident.tile([P, PASSES, FEATURES], U32, align_bytes=64)
+        da_scales = resident.tile([P, PASSES, FEATURES], U8, align_bytes=64)
+        z_codes = resident.tile([P, PASSES, FEATURES], U32, align_bytes=64)
+        z_scales = resident.tile([P, PASSES, FEATURES], U8, align_bytes=64)
+
+        def load(tile, dram, first_row, c, rows):
+            start = first_row + c * K_PASS
+            view = dram[start : start + K_PASS, :].rearrange("(p j) w -> p j w", j=PACK)
+            nc.sync.dma_start(out=tile[c][:, rows, :], in_=view[:, rows, :])
+
+        def load_da_inputs(c):
+            for rows in halves:
+                load(cell_t, cell, 0, c, rows)
+                load(gh_t, grad_rows, TOKENS, c, rows)
+                load(o_t, gate_o, 0, c, rows)
+                load(gc_t, grad_rows, 0, c, rows)
+            for rows in halves:
+                load(f_t, gate_f, 0, c, rows)
+
+        def load_z_inputs(c):
+            for rows in halves:
+                load(x_t, inputs, 0, c, rows)
+                load(h_t, short_term_memory, 0, c, rows)
+
+        def minus_dc(c, rows):
+            cl, o = cell_t[c][:, rows, :], o_t[c][:, rows, :]
+            nc.scalar.activation(out=cl, in_=cl, func=ACT.Tanh)
+            nc.scalar.activation(out=cl, in_=cl, func=ACT.Square)
+            nc.vector.tensor_tensor(out=o, in0=o, in1=gh_t[c][:, rows, :], op=ALU.mult)
+            nc.vector.scalar_tensor_tensor(
+                out=o, in0=cl, scalar=1.0, in1=o, op0=ALU.subtract, op1=ALU.mult
+            )
+            nc.vector.tensor_tensor(out=o, in0=o, in1=gc_t[c][:, rows, :], op=ALU.subtract)
+
+        def quantise_da(c):
+            for rows in halves:
+                f = f_t[c][:, rows, :]
+                nc.scalar.activation(out=f, in_=f, func=ACT.Square, bias=-0.5)
+            for k in range(FEATURES // DA_COLS):
+                cols = slice(k * DA_COLS, (k + 1) * DA_COLS)
+                da_grouped = grouped.tile([P, DA_COLS, PACK], BF16, align_bytes=64)
+                nc.vector.scalar_tensor_tensor(
+                    out=da_grouped[:],
+                    in0=f_t[c][:, :, cols].rearrange("p j w -> p w j"),
+                    scalar=0.25,
+                    in1=o_t[c][:, :, cols].rearrange("p j w -> p w j"),
+                    op0=ALU.subtract,
+                    op1=ALU.mult,
+                )
+                nc.vector.quantize_mx(
+                    out=da_codes[:, c, cols].bitcast(E5M2_X4),
+                    scales=da_scales[:, c, cols],
+                    in_=da_grouped[:].rearrange("p w j -> p (w j)"),
+                )
+
+        def quantise_z(c):
+            for rows in halves:
+                x = x_t[c][:, rows, :]
+                nc.vector.tensor_tensor(out=x, in0=x, in1=h_t[c][:, rows, :], op=ALU.add)
+            for k in range(FEATURES // Z_COLS):
+                cols = slice(k * Z_COLS, (k + 1) * Z_COLS)
+                z_grouped = grouped.tile([P, Z_COLS, PACK], BF16, align_bytes=64)
+                nc.scalar.copy(
+                    out=z_grouped[:], in_=x_t[c][:, :, cols].rearrange("p j w -> p w j")
+                )
+                nc.vector.quantize_mx(
+                    out=z_codes[:, c, cols].bitcast(E4M3_X4),
+                    scales=z_scales[:, c, cols],
+                    in_=z_grouped[:].rearrange("p w j -> p (w j)"),
+                )
+
+        def multiply(acc, m, n, c):
+            m_cols = slice(m * M_TILE, (m + 1) * M_TILE)
+            n_cols = slice(n * N_TILE, (n + 1) * N_TILE)
+            nc.tensor.matmul_mx(
+                out=acc[:],
+                lhsT=da_codes[:, c, m_cols].bitcast(E5M2_X4),
+                lhsT_scale=da_scales[:, c, m_cols],
+                rhs=z_codes[:, c, n_cols].bitcast(E4M3_X4),
+                rhs_scale=z_scales[:, c, n_cols],
+                start=(c == 0),
+                stop=(c == PASSES - 1),
+            )
+
+        def store(m, accs, second_engine_copy):
+            result = results.tile([P, FEATURES], F32)
+            nc.scalar.copy(out=result[:, 0:N_TILE], in_=accs[0][:])
+            second_engine_copy(out=result[:, N_TILE : 2 * N_TILE], in_=accs[1][:])
+            nc.sync.dma_start(out=out[m * M_TILE : (m + 1) * M_TILE, :], in_=result[:])
+
+        load_da_inputs(0)
+        load_z_inputs(0)
+        load_z_inputs(1)
+        load_da_inputs(1)
+
+        for rows in halves:
+            minus_dc(0, rows)
+        quantise_da(0)
+        quantise_z(0)
+
+        early = {}
+        for m in range(EARLY_M_TILES):
+            for n in range(N_TILES):
+                early[(m, n)] = psum.tile([P, N_TILE], F32, name="acc")
+                multiply(early[(m, n)], m, n, 0)
+
+        quantise_z(1)
+        for rows in halves:
+            minus_dc(1, rows)
+        quantise_da(1)
+
+        for m in range(EARLY_M_TILES):
+            for n in range(N_TILES):
+                multiply(early[(m, n)], m, n, 1)
+            store(m, [early[(m, n)] for n in range(N_TILES)], nc.scalar.copy)
+
+        for m in range(EARLY_M_TILES, M_TILES):
+            accs = []
+            for n in range(N_TILES):
+                acc = psum.tile([P, N_TILE], F32, name="acc")
+                for c in range(PASSES):
+                    multiply(acc, m, n, c)
+                accs.append(acc)
+            store(m, accs, nc.vector.tensor_copy)

@@ -18,6 +18,8 @@ PASSES = TOKENS // K_PASS
 HALF_ROWS = PACK // 2
 DA_COLS = 256
 Z_COLS = 512
+DA_CHUNKS = FEATURES // DA_COLS
+Z_CHUNKS = FEATURES // Z_COLS
 M_TILE = 128
 N_TILE = 512
 M_TILES = FEATURES // M_TILE
@@ -50,6 +52,7 @@ def tile_lstmcell_pa_v_kernel(
     nc = tc.nc
     grad_rows = grad_out.flatten_outer_dims()
     halves = [slice(u * HALF_ROWS, (u + 1) * HALF_ROWS) for u in range(PACK // HALF_ROWS)]
+    all_rows = slice(0, PACK)
 
     with (
         tc.tile_pool(name="resident", bufs=1) as resident,
@@ -91,56 +94,69 @@ def tile_lstmcell_pa_v_kernel(
                 load(f_t, gate_f, 0, c, rows)
 
         def load_z_inputs(c):
-            for rows in halves:
-                load(x_t, inputs, 0, c, rows)
-                load(h_t, short_term_memory, 0, c, rows)
+            load(x_t, inputs, 0, c, all_rows)
+            load(h_t, short_term_memory, 0, c, all_rows)
+
+        def tanh_squared(c, rows):
+            cl = cell_t[c][:, rows, :]
+            nc.scalar.activation(out=cl, in_=cl, func=ACT.Tanh)
+            nc.scalar.activation(out=cl, in_=cl, func=ACT.Square)
 
         def minus_dc(c, rows):
             cl, o = cell_t[c][:, rows, :], o_t[c][:, rows, :]
-            nc.scalar.activation(out=cl, in_=cl, func=ACT.Tanh)
-            nc.scalar.activation(out=cl, in_=cl, func=ACT.Square)
             nc.vector.tensor_tensor(out=o, in0=o, in1=gh_t[c][:, rows, :], op=ALU.mult)
             nc.vector.scalar_tensor_tensor(
                 out=o, in0=cl, scalar=1.0, in1=o, op0=ALU.subtract, op1=ALU.mult
             )
             nc.vector.tensor_tensor(out=o, in0=o, in1=gc_t[c][:, rows, :], op=ALU.subtract)
 
-        def quantise_da(c):
-            for rows in halves:
-                f = f_t[c][:, rows, :]
-                nc.scalar.activation(out=f, in_=f, func=ACT.Square, bias=-0.5)
-            for k in range(FEATURES // DA_COLS):
-                cols = slice(k * DA_COLS, (k + 1) * DA_COLS)
-                da_grouped = grouped.tile([P, DA_COLS, PACK], BF16, align_bytes=64)
-                nc.vector.scalar_tensor_tensor(
-                    out=da_grouped[:],
-                    in0=f_t[c][:, :, cols].rearrange("p j w -> p w j"),
-                    scalar=0.25,
-                    in1=o_t[c][:, :, cols].rearrange("p j w -> p w j"),
-                    op0=ALU.subtract,
-                    op1=ALU.mult,
-                )
-                nc.vector.quantize_mx(
-                    out=da_codes[:, c, cols].bitcast(E5M2_X4),
-                    scales=da_scales[:, c, cols],
-                    in_=da_grouped[:].rearrange("p w j -> p (w j)"),
-                )
+        def da_cols(k):
+            return slice(k * DA_COLS, (k + 1) * DA_COLS)
 
-        def quantise_z(c):
-            for rows in halves:
-                x = x_t[c][:, rows, :]
-                nc.vector.tensor_tensor(out=x, in0=x, in1=h_t[c][:, rows, :], op=ALU.add)
-            for k in range(FEATURES // Z_COLS):
-                cols = slice(k * Z_COLS, (k + 1) * Z_COLS)
-                z_grouped = grouped.tile([P, Z_COLS, PACK], BF16, align_bytes=64)
-                nc.scalar.copy(
-                    out=z_grouped[:], in_=x_t[c][:, :, cols].rearrange("p j w -> p w j")
-                )
-                nc.vector.quantize_mx(
-                    out=z_codes[:, c, cols].bitcast(E4M3_X4),
-                    scales=z_scales[:, c, cols],
-                    in_=z_grouped[:].rearrange("p w j -> p (w j)"),
-                )
+        def z_cols(k):
+            return slice(k * Z_COLS, (k + 1) * Z_COLS)
+
+        def centred_f_squared(c, k):
+            f = f_t[c][:, :, da_cols(k)]
+            nc.scalar.activation(out=f, in_=f, func=ACT.Square, bias=-0.5)
+
+        def quantise_da(c, k):
+            cols = da_cols(k)
+            da_grouped = grouped.tile([P, DA_COLS, PACK], BF16, align_bytes=64)
+            nc.vector.scalar_tensor_tensor(
+                out=da_grouped[:],
+                in0=f_t[c][:, :, cols].rearrange("p j w -> p w j"),
+                scalar=0.25,
+                in1=o_t[c][:, :, cols].rearrange("p j w -> p w j"),
+                op0=ALU.subtract,
+                op1=ALU.mult,
+            )
+            nc.vector.quantize_mx(
+                out=da_codes[:, c, cols].bitcast(E5M2_X4),
+                scales=da_scales[:, c, cols],
+                in_=da_grouped[:].rearrange("p w j -> p (w j)"),
+            )
+
+        def add_z(c):
+            for k in range(Z_CHUNKS):
+                x = x_t[c][:, :, z_cols(k)]
+                nc.vector.tensor_tensor(out=x, in0=x, in1=h_t[c][:, :, z_cols(k)], op=ALU.add)
+
+        z_grouped = {}
+
+        def regroup_z(c, k):
+            z_grouped[(c, k)] = grouped.tile([P, Z_COLS, PACK], BF16, align_bytes=64, name="z_grouped")
+            nc.scalar.copy(
+                out=z_grouped[(c, k)][:],
+                in_=x_t[c][:, :, z_cols(k)].rearrange("p j w -> p w j"),
+            )
+
+        def quantise_z(c, k):
+            nc.vector.quantize_mx(
+                out=z_codes[:, c, z_cols(k)].bitcast(E4M3_X4),
+                scales=z_scales[:, c, z_cols(k)],
+                in_=z_grouped[(c, k)][:].rearrange("p w j -> p (w j)"),
+            )
 
         def multiply(acc, m, n, c):
             m_cols = slice(m * M_TILE, (m + 1) * M_TILE)
@@ -161,37 +177,57 @@ def tile_lstmcell_pa_v_kernel(
             second_engine_copy(out=result[:, N_TILE : 2 * N_TILE], in_=accs[1][:])
             nc.sync.dma_start(out=out[m * M_TILE : (m + 1) * M_TILE, :], in_=result[:])
 
-        load_da_inputs(0)
-        load_z_inputs(0)
-        load_z_inputs(1)
-        load_da_inputs(1)
+        with tc.manual_schedule():
+            load_da_inputs(0)
+            load_z_inputs(0)
+            load_z_inputs(1)
+            load_da_inputs(1)
 
-        for rows in halves:
-            minus_dc(0, rows)
-        quantise_da(0)
-        quantise_z(0)
+            for rows in halves:
+                tanh_squared(0, rows)
+                minus_dc(0, rows)
+            for k in range(DA_CHUNKS):
+                centred_f_squared(0, k)
+            for k in range(DA_CHUNKS // 2):
+                quantise_da(0, k)
+            add_z(0)
+            for k in range(DA_CHUNKS // 2, DA_CHUNKS):
+                quantise_da(0, k)
+            add_z(1)
+            regroup_z(0, 0)
+            regroup_z(0, 1)
+            regroup_z(1, 0)
+            quantise_z(0, 0)
+            quantise_z(0, 1)
 
-        early = {}
-        for m in range(EARLY_M_TILES):
-            for n in range(N_TILES):
-                early[(m, n)] = psum.tile([P, N_TILE], F32, name="acc")
-                multiply(early[(m, n)], m, n, 0)
+            early = {}
+            for m in range(EARLY_M_TILES):
+                for n in range(N_TILES):
+                    early[(m, n)] = psum.tile([P, N_TILE], F32, name="acc")
+                    multiply(early[(m, n)], m, n, 0)
 
-        quantise_z(1)
-        for rows in halves:
-            minus_dc(1, rows)
-        quantise_da(1)
+            tanh_squared(1, halves[0])
+            regroup_z(1, 1)
+            tanh_squared(1, halves[1])
+            minus_dc(1, halves[0])
+            quantise_z(1, 0)
+            quantise_z(1, 1)
+            minus_dc(1, halves[1])
+            for k in range(DA_CHUNKS):
+                centred_f_squared(1, k)
+            for k in range(DA_CHUNKS):
+                quantise_da(1, k)
 
-        for m in range(EARLY_M_TILES):
-            for n in range(N_TILES):
-                multiply(early[(m, n)], m, n, 1)
-            store(m, [early[(m, n)] for n in range(N_TILES)], nc.scalar.copy)
+            for m in range(EARLY_M_TILES):
+                for n in range(N_TILES):
+                    multiply(early[(m, n)], m, n, 1)
+                store(m, [early[(m, n)] for n in range(N_TILES)], nc.scalar.copy)
 
-        for m in range(EARLY_M_TILES, M_TILES):
-            accs = []
-            for n in range(N_TILES):
-                acc = psum.tile([P, N_TILE], F32, name="acc")
-                for c in range(PASSES):
-                    multiply(acc, m, n, c)
-                accs.append(acc)
-            store(m, accs, nc.vector.tensor_copy)
+            for m in range(EARLY_M_TILES, M_TILES):
+                accs = []
+                for n in range(N_TILES):
+                    acc = psum.tile([P, N_TILE], F32, name="acc")
+                    for c in range(PASSES):
+                        multiply(acc, m, n, c)
+                    accs.append(acc)
+                store(m, accs, nc.vector.tensor_copy)

@@ -51,8 +51,8 @@ def tile_lstmcell_pa_v_kernel(
 ):
     nc = tc.nc
     grad_rows = grad_out.flatten_outer_dims()
-    halves = [slice(u * HALF_ROWS, (u + 1) * HALF_ROWS) for u in range(PACK // HALF_ROWS)]
-    all_rows = slice(0, PACK)
+    halves = [range(u * HALF_ROWS, (u + 1) * HALF_ROWS) for u in range(PACK // HALF_ROWS)]
+    all_rows = range(PACK)
 
     with (
         tc.tile_pool(name="resident", bufs=1) as resident,
@@ -82,7 +82,8 @@ def tile_lstmcell_pa_v_kernel(
         def load(tile, dram, first_row, c, rows):
             start = first_row + c * K_PASS
             view = dram[start : start + K_PASS, :].rearrange("(p j) w -> p j w", j=PACK)
-            nc.sync.dma_start(out=tile[c][:, rows, :], in_=view[:, rows, :])
+            js = slice(rows[0], rows[-1] + 1)
+            nc.sync.dma_start(out=tile[c][:, js, :], in_=view[:, js, :])
 
         def load_da_inputs(c):
             for rows in halves:
@@ -98,17 +99,22 @@ def tile_lstmcell_pa_v_kernel(
             load(h_t, short_term_memory, 0, c, all_rows)
 
         def tanh_squared(c, rows):
-            cl = cell_t[c][:, rows, :]
-            nc.scalar.activation(out=cl, in_=cl, func=ACT.Tanh)
-            nc.scalar.activation(out=cl, in_=cl, func=ACT.Square)
+            for func in (ACT.Tanh, ACT.Square):
+                for j in rows:
+                    nc.scalar.activation(out=cell_t[c][:, j, :], in_=cell_t[c][:, j, :], func=func)
 
         def minus_dc(c, rows):
-            cl, o = cell_t[c][:, rows, :], o_t[c][:, rows, :]
-            nc.vector.tensor_tensor(out=o, in0=o, in1=gh_t[c][:, rows, :], op=ALU.mult)
-            nc.vector.scalar_tensor_tensor(
-                out=o, in0=cl, scalar=1.0, in1=o, op0=ALU.subtract, op1=ALU.mult
-            )
-            nc.vector.tensor_tensor(out=o, in0=o, in1=gc_t[c][:, rows, :], op=ALU.subtract)
+            for j in rows:
+                o = o_t[c][:, j, :]
+                nc.vector.tensor_tensor(out=o, in0=o, in1=gh_t[c][:, j, :], op=ALU.mult)
+            for j in rows:
+                o = o_t[c][:, j, :]
+                nc.vector.scalar_tensor_tensor(
+                    out=o, in0=cell_t[c][:, j, :], scalar=1.0, in1=o, op0=ALU.subtract, op1=ALU.mult
+                )
+            for j in rows:
+                o = o_t[c][:, j, :]
+                nc.vector.tensor_tensor(out=o, in0=o, in1=gc_t[c][:, j, :], op=ALU.subtract)
 
         def da_cols(k):
             return slice(k * DA_COLS, (k + 1) * DA_COLS)
@@ -120,22 +126,33 @@ def tile_lstmcell_pa_v_kernel(
             f = f_t[c][:, :, da_cols(k)]
             nc.scalar.activation(out=f, in_=f, func=ACT.Square, bias=-0.5)
 
-        def quantise_da(c, k):
+        da_grouped = {}
+
+        def form_da(c, k):
             cols = da_cols(k)
-            da_grouped = grouped.tile([P, DA_COLS, PACK], BF16, align_bytes=64)
+            da_grouped[(c, k)] = grouped.tile([P, DA_COLS, PACK], BF16, align_bytes=64, name="da_grouped")
             nc.vector.scalar_tensor_tensor(
-                out=da_grouped[:],
+                out=da_grouped[(c, k)][:],
                 in0=f_t[c][:, :, cols].rearrange("p j w -> p w j"),
                 scalar=0.25,
                 in1=o_t[c][:, :, cols].rearrange("p j w -> p w j"),
                 op0=ALU.subtract,
                 op1=ALU.mult,
             )
+
+        def quantise_da(c, k):
             nc.vector.quantize_mx(
-                out=da_codes[:, c, cols].bitcast(E5M2_X4),
-                scales=da_scales[:, c, cols],
-                in_=da_grouped[:].rearrange("p w j -> p (w j)"),
+                out=da_codes[:, c, da_cols(k)].bitcast(E5M2_X4),
+                scales=da_scales[:, c, da_cols(k)],
+                in_=da_grouped[(c, k)][:].rearrange("p w j -> p (w j)"),
             )
+
+        def form_and_quantise_da(c, chunks):
+            for k in chunks:
+                form_da(c, k)
+                if k > chunks[0]:
+                    quantise_da(c, k - 1)
+            quantise_da(c, chunks[-1])
 
         def add_z(c):
             for k in range(Z_CHUNKS):
@@ -188,17 +205,14 @@ def tile_lstmcell_pa_v_kernel(
                 minus_dc(0, rows)
             for k in range(DA_CHUNKS):
                 centred_f_squared(0, k)
-            for k in range(DA_CHUNKS // 2):
-                quantise_da(0, k)
+            form_and_quantise_da(0, range(0, DA_CHUNKS // 2))
             add_z(0)
-            for k in range(DA_CHUNKS // 2, DA_CHUNKS):
-                quantise_da(0, k)
+            form_and_quantise_da(0, range(DA_CHUNKS // 2, DA_CHUNKS))
             add_z(1)
-            regroup_z(0, 0)
-            regroup_z(0, 1)
-            regroup_z(1, 0)
-            quantise_z(0, 0)
-            quantise_z(0, 1)
+            for k in range(Z_CHUNKS):
+                regroup_z(0, k)
+            for k in range(Z_CHUNKS):
+                quantise_z(0, k)
 
             early = {}
             for m in range(EARLY_M_TILES):
@@ -207,16 +221,16 @@ def tile_lstmcell_pa_v_kernel(
                     multiply(early[(m, n)], m, n, 0)
 
             tanh_squared(1, halves[0])
-            regroup_z(1, 1)
+            for k in range(Z_CHUNKS):
+                regroup_z(1, k)
             tanh_squared(1, halves[1])
             minus_dc(1, halves[0])
-            quantise_z(1, 0)
-            quantise_z(1, 1)
+            for k in range(Z_CHUNKS):
+                quantise_z(1, k)
             minus_dc(1, halves[1])
             for k in range(DA_CHUNKS):
                 centred_f_squared(1, k)
-            for k in range(DA_CHUNKS):
-                quantise_da(1, k)
+            form_and_quantise_da(1, range(DA_CHUNKS))
 
             for m in range(EARLY_M_TILES):
                 for n in range(N_TILES):

@@ -16,9 +16,12 @@ TOKENS = 1024
 FEATURES = 1024
 PASSES = TOKENS // K_PASS
 HALF_ROWS = PACK // 2
-DA_COLS = 256
+DA_COLS = 128
+F_COLS = 256
 Z_COLS = 512
+RUN = 4
 DA_CHUNKS = FEATURES // DA_COLS
+F_CHUNKS = FEATURES // F_COLS
 Z_CHUNKS = FEATURES // Z_COLS
 M_TILE = 128
 N_TILE = 512
@@ -123,7 +126,7 @@ def tile_lstmcell_pa_v_kernel(
             return slice(k * Z_COLS, (k + 1) * Z_COLS)
 
         def centred_f_squared(c, k):
-            f = f_t[c][:, :, da_cols(k)]
+            f = f_t[c][:, :, k * F_COLS : (k + 1) * F_COLS]
             nc.scalar.activation(out=f, in_=f, func=ACT.Square, bias=-0.5)
 
         da_grouped = {}
@@ -164,8 +167,8 @@ def tile_lstmcell_pa_v_kernel(
         def regroup_z(c, k):
             z_grouped[(c, k)] = grouped.tile([P, Z_COLS, PACK], BF16, align_bytes=64, name="z_grouped")
             nc.scalar.copy(
-                out=z_grouped[(c, k)][:],
-                in_=x_t[c][:, :, z_cols(k)].rearrange("p j w -> p w j"),
+                out=z_grouped[(c, k)][:].rearrange("p (g i) j -> p g j i", i=RUN),
+                in_=x_t[c][:, :, z_cols(k)].rearrange("p j (g i) -> p g j i", i=RUN),
             )
 
         def quantise_z(c, k):
@@ -203,7 +206,7 @@ def tile_lstmcell_pa_v_kernel(
             for rows in halves:
                 tanh_squared(0, rows)
                 minus_dc(0, rows)
-            for k in range(DA_CHUNKS):
+            for k in range(F_CHUNKS):
                 centred_f_squared(0, k)
             form_and_quantise_da(0, range(0, DA_CHUNKS // 2))
             add_z(0)
@@ -228,7 +231,7 @@ def tile_lstmcell_pa_v_kernel(
             for k in range(Z_CHUNKS):
                 quantise_z(1, k)
             minus_dc(1, halves[1])
-            for k in range(DA_CHUNKS):
+            for k in range(F_CHUNKS):
                 centred_f_squared(1, k)
             form_and_quantise_da(1, range(DA_CHUNKS))
 

@@ -17,6 +17,7 @@ FEATURES = 1024
 PASSES = TOKENS // K_PASS
 HALF_ROWS = PACK // 2
 DA_COLS = 128
+WIDE_DA_COLS = 256
 F_COLS = 256
 Z_COLS = 512
 RUN = 4
@@ -94,8 +95,7 @@ def tile_lstmcell_pa_v_kernel(
                 load(gh_t, grad_rows, TOKENS, c, rows)
                 load(o_t, gate_o, 0, c, rows)
                 load(gc_t, grad_rows, 0, c, rows)
-            for rows in halves:
-                load(f_t, gate_f, 0, c, rows)
+            load(f_t, gate_f, 0, c, all_rows)
 
         def load_z_inputs(c):
             load(x_t, inputs, 0, c, all_rows)
@@ -119,8 +119,8 @@ def tile_lstmcell_pa_v_kernel(
                 o = o_t[c][:, j, :]
                 nc.vector.tensor_tensor(out=o, in0=o, in1=gc_t[c][:, j, :], op=ALU.subtract)
 
-        def da_cols(k):
-            return slice(k * DA_COLS, (k + 1) * DA_COLS)
+        def da_cols(k, width):
+            return slice(k * width, (k + 1) * width)
 
         def z_cols(k):
             return slice(k * Z_COLS, (k + 1) * Z_COLS)
@@ -131,9 +131,9 @@ def tile_lstmcell_pa_v_kernel(
 
         da_grouped = {}
 
-        def form_da(c, k):
-            cols = da_cols(k)
-            da_grouped[(c, k)] = grouped.tile([P, DA_COLS, PACK], BF16, align_bytes=64, name="da_grouped")
+        def form_da(c, k, width):
+            cols = da_cols(k, width)
+            da_grouped[(c, k)] = grouped.tile([P, width, PACK], BF16, align_bytes=64, name="da_grouped")
             nc.vector.scalar_tensor_tensor(
                 out=da_grouped[(c, k)][:],
                 in0=f_t[c][:, :, cols].rearrange("p j w -> p w j"),
@@ -143,19 +143,19 @@ def tile_lstmcell_pa_v_kernel(
                 op1=ALU.mult,
             )
 
-        def quantise_da(c, k):
+        def quantise_da(c, k, width):
             nc.vector.quantize_mx(
-                out=da_codes[:, c, da_cols(k)].bitcast(E5M2_X4),
-                scales=da_scales[:, c, da_cols(k)],
+                out=da_codes[:, c, da_cols(k, width)].bitcast(E5M2_X4),
+                scales=da_scales[:, c, da_cols(k, width)],
                 in_=da_grouped[(c, k)][:].rearrange("p w j -> p (w j)"),
             )
 
-        def form_and_quantise_da(c, chunks):
+        def form_and_quantise_da(c, chunks, width):
             for k in chunks:
-                form_da(c, k)
+                form_da(c, k, width)
                 if k > chunks[0]:
-                    quantise_da(c, k - 1)
-            quantise_da(c, chunks[-1])
+                    quantise_da(c, k - 1, width)
+            quantise_da(c, chunks[-1], width)
 
         def add_z(c):
             for k in range(Z_CHUNKS):
@@ -208,9 +208,9 @@ def tile_lstmcell_pa_v_kernel(
                 minus_dc(0, rows)
             for k in range(F_CHUNKS):
                 centred_f_squared(0, k)
-            form_and_quantise_da(0, range(0, DA_CHUNKS // 2))
+            form_and_quantise_da(0, range(0, 2), WIDE_DA_COLS)
             add_z(0)
-            form_and_quantise_da(0, range(DA_CHUNKS // 2, DA_CHUNKS))
+            form_and_quantise_da(0, range(2, 4), WIDE_DA_COLS)
             add_z(1)
             for k in range(Z_CHUNKS):
                 regroup_z(0, k)
@@ -233,7 +233,7 @@ def tile_lstmcell_pa_v_kernel(
             minus_dc(1, halves[1])
             for k in range(F_CHUNKS):
                 centred_f_squared(1, k)
-            form_and_quantise_da(1, range(DA_CHUNKS))
+            form_and_quantise_da(1, range(DA_CHUNKS), DA_COLS)
 
             for m in range(EARLY_M_TILES):
                 for n in range(N_TILES):

@@ -16,20 +16,16 @@ TOKENS = 1024
 FEATURES = 1024
 PASSES = TOKENS // K_PASS
 HALF_ROWS = PACK // 2
-DA_COLS = 128
-WIDE_DA_COLS = 256
-F_COLS = 256
+DA_COLS = 256
 Z_COLS = 512
 RUN = 4
 DA_CHUNKS = FEATURES // DA_COLS
-F_CHUNKS = FEATURES // F_COLS
 Z_CHUNKS = FEATURES // Z_COLS
 M_TILE = 128
 N_TILE = 512
 M_TILES = FEATURES // M_TILE
 N_TILES = FEATURES // N_TILE
 PSUM_BANKS = 8
-EARLY_M_TILES = PSUM_BANKS // N_TILES
 
 FLOPS = 2 * TOKENS * FEATURES * FEATURES
 BYTES = TOKENS * FEATURES * (2 + 2 + 4 + 4 + 4 + 2 + 2) + FEATURES * FEATURES * 4
@@ -61,7 +57,7 @@ def tile_lstmcell_pa_v_kernel(
     with (
         tc.tile_pool(name="resident", bufs=1) as resident,
         tc.tile_pool(name="grouped", bufs=3) as grouped,
-        tc.tile_pool(name="results", bufs=4) as results,
+        tc.tile_pool(name="results", bufs=6) as results,
         tc.psum_pool(name="psum", bufs=PSUM_BANKS) as psum,
     ):
         def pass_tiles(name, dtype):
@@ -72,11 +68,16 @@ def tile_lstmcell_pa_v_kernel(
 
         cell_t = pass_tiles("cell", F32)
         o_t = pass_tiles("gate_o", F32)
-        f_t = pass_tiles("gate_f", F32)
+        f_t = [
+            resident.tile([P, PACK, FEATURES], F32, name="gate_f0"),
+            None,
+        ]
+        f1_t = [resident.tile([P, PACK, FEATURES // 2], F32, name="gate_f1_%d" % u) for u in range(2)]
         gc_t = pass_tiles("grad_c", BF16)
         gh_t = pass_tiles("grad_h", BF16)
         x_t = pass_tiles("x", BF16)
         h_t = pass_tiles("h", BF16)
+
 
         da_codes = resident.tile([P, PASSES, FEATURES], U32, align_bytes=64)
         da_scales = resident.tile([P, PASSES, FEATURES], U8, align_bytes=64)
@@ -89,15 +90,27 @@ def tile_lstmcell_pa_v_kernel(
             js = slice(rows[0], rows[-1] + 1)
             nc.sync.dma_start(out=tile[c][:, js, :], in_=view[:, js, :])
 
-        def load_da_inputs(c):
-            for rows in halves:
-                load(cell_t, cell, 0, c, rows)
-                load(gh_t, grad_rows, TOKENS, c, rows)
-                load(o_t, gate_o, 0, c, rows)
-                load(gc_t, grad_rows, 0, c, rows)
+        def load_cell(c, rows):
+            load(cell_t, cell, 0, c, rows)
+
+        def load_gh(c, rows):
+            load(gh_t, grad_rows, TOKENS, c, rows)
+
+        def load_o(c, rows):
+            load(o_t, gate_o, 0, c, rows)
+
+        def load_gc(c, rows):
+            load(gc_t, grad_rows, 0, c, rows)
+
+        def load_f(c):
             load(f_t, gate_f, 0, c, all_rows)
 
-        def load_z_inputs(c):
+        def load_f_half(c, u):
+            cols = slice(u * 512, (u + 1) * 512)
+            view = gate_f[c * K_PASS : (c + 1) * K_PASS, :].rearrange("(p j) w -> p j w", j=PACK)
+            nc.sync.dma_start(out=f1_t[u][:], in_=view[:, :, cols])
+
+        def load_z(c):
             load(x_t, inputs, 0, c, all_rows)
             load(h_t, short_term_memory, 0, c, all_rows)
 
@@ -106,56 +119,98 @@ def tile_lstmcell_pa_v_kernel(
                 for j in rows:
                     nc.scalar.activation(out=cell_t[c][:, j, :], in_=cell_t[c][:, j, :], func=func)
 
-        def minus_dc(c, rows):
+        def times_gh(c, rows):
             for j in rows:
                 o = o_t[c][:, j, :]
                 nc.vector.tensor_tensor(out=o, in0=o, in1=gh_t[c][:, j, :], op=ALU.mult)
+
+        def times_tanh(c, rows):
             for j in rows:
                 o = o_t[c][:, j, :]
                 nc.vector.scalar_tensor_tensor(
                     out=o, in0=cell_t[c][:, j, :], scalar=1.0, in1=o, op0=ALU.subtract, op1=ALU.mult
                 )
-            for j in rows:
-                o = o_t[c][:, j, :]
-                nc.vector.tensor_tensor(out=o, in0=o, in1=gc_t[c][:, j, :], op=ALU.subtract)
 
-        def da_cols(k, width):
-            return slice(k * width, (k + 1) * width)
+        def da_cols(k):
+            return slice(k * DA_COLS, (k + 1) * DA_COLS)
 
         def z_cols(k):
             return slice(k * Z_COLS, (k + 1) * Z_COLS)
 
-        def centred_f_squared(c, k):
-            f = f_t[c][:, :, k * F_COLS : (k + 1) * F_COLS]
+        def f_squared_rows(c, k):
+            if c == 0:
+                f = f_t[c][:, :, da_cols(k)]
+            else:
+                f = f1_t[k // 2][:, :, da_cols(k % 2)]
             nc.scalar.activation(out=f, in_=f, func=ACT.Square, bias=-0.5)
 
-        da_grouped = {}
+        def minus_dc_rows(c, rows):
+            for j in rows:
+                o = o_t[c][:, j, :]
+                nc.vector.tensor_tensor(out=o, in0=o, in1=gc_t[c][:, j, :], op=ALU.subtract)
 
-        def form_da(c, k, width):
-            cols = da_cols(k, width)
-            da_grouped[(c, k)] = grouped.tile([P, width, PACK], BF16, align_bytes=64, name="da_grouped")
+        def minus_dc_half(c, rows, u):
+            js = slice(rows[0], rows[-1] + 1)
+            o = o_t[c][:, js, u * 512 : (u + 1) * 512]
+            nc.vector.tensor_tensor(out=o, in0=o, in1=gc_t[c][:, js, u * 512 : (u + 1) * 512], op=ALU.subtract)
+
+        da_g = {}
+
+        def times_gh_half(c, rows, u):
+            js = slice(rows[0], rows[-1] + 1)
+            o = o_t[c][:, js, u * 512 : (u + 1) * 512]
+            nc.vector.tensor_tensor(out=o, in0=o, in1=gh_t[c][:, js, u * 512 : (u + 1) * 512], op=ALU.mult)
+
+        def times_tanh_half(c, rows, u):
+            js = slice(rows[0], rows[-1] + 1)
+            o = o_t[c][:, js, u * 512 : (u + 1) * 512]
             nc.vector.scalar_tensor_tensor(
-                out=da_grouped[(c, k)][:],
-                in0=f_t[c][:, :, cols].rearrange("p j w -> p w j"),
+                out=o, in0=cell_t[c][:, js, u * 512 : (u + 1) * 512], scalar=1.0, in1=o, op0=ALU.subtract, op1=ALU.mult
+            )
+
+        def form_m(c, m):
+            cols = slice(m * M_TILE, (m + 1) * M_TILE)
+            da_g[(c, m)] = grouped.tile([P, M_TILE, PACK], BF16, align_bytes=64, name="da_g")
+            nc.vector.scalar_tensor_tensor(
+                out=da_g[(c, m)][:],
+                in0=f1_t[m // 4][:, :, (m % 4) * M_TILE : (m % 4 + 1) * M_TILE].rearrange("p j w -> p w j"),
                 scalar=0.25,
                 in1=o_t[c][:, :, cols].rearrange("p j w -> p w j"),
                 op0=ALU.subtract,
                 op1=ALU.mult,
             )
 
-        def quantise_da(c, k, width):
+        def quant_m(c, m):
+            cols = slice(m * M_TILE, (m + 1) * M_TILE)
             nc.vector.quantize_mx(
-                out=da_codes[:, c, da_cols(k, width)].bitcast(E5M2_X4),
-                scales=da_scales[:, c, da_cols(k, width)],
-                in_=da_grouped[(c, k)][:].rearrange("p w j -> p (w j)"),
+                out=da_codes[:, c, cols].bitcast(E5M2_X4),
+                scales=da_scales[:, c, cols],
+                in_=da_g[(c, m)][:].rearrange("p w j -> p (w j)"),
             )
 
-        def form_and_quantise_da(c, chunks, width):
-            for k in chunks:
-                form_da(c, k, width)
-                if k > chunks[0]:
-                    quantise_da(c, k - 1, width)
-            quantise_da(c, chunks[-1], width)
+        def add_zk(c, k):
+            x = x_t[c][:, :, z_cols(k)]
+            nc.vector.tensor_tensor(out=x, in0=x, in1=h_t[c][:, :, z_cols(k)], op=ALU.add)
+
+        def form_da_rows(c, k):
+            da_grouped[(c, k)] = grouped.tile([P, DA_COLS, PACK], BF16, align_bytes=64, name="da_grouped")
+            nc.vector.scalar_tensor_tensor(
+                out=da_grouped[(c, k)][:],
+                in0=f_t[c][:, :, da_cols(k)].rearrange("p j w -> p w j"),
+                scalar=0.25,
+                in1=o_t[c][:, :, da_cols(k)].rearrange("p j w -> p w j"),
+                op0=ALU.subtract,
+                op1=ALU.mult,
+            )
+
+        da_grouped = {}
+
+        def quantise_da(c, k):
+            nc.vector.quantize_mx(
+                out=da_codes[:, c, da_cols(k)].bitcast(E5M2_X4),
+                scales=da_scales[:, c, da_cols(k)],
+                in_=da_grouped[(c, k)][:].rearrange("p w j -> p (w j)"),
+            )
 
         def add_z(c):
             for k in range(Z_CHUNKS):
@@ -178,73 +233,131 @@ def tile_lstmcell_pa_v_kernel(
                 in_=z_grouped[(c, k)][:].rearrange("p w j -> p (w j)"),
             )
 
-        def multiply(acc, m, n, c):
-            m_cols = slice(m * M_TILE, (m + 1) * M_TILE)
-            n_cols = slice(n * N_TILE, (n + 1) * N_TILE)
-            nc.tensor.matmul_mx(
-                out=acc[:],
-                lhsT=da_codes[:, c, m_cols].bitcast(E5M2_X4),
-                lhsT_scale=da_scales[:, c, m_cols],
-                rhs=z_codes[:, c, n_cols].bitcast(E4M3_X4),
-                rhs_scale=z_scales[:, c, n_cols],
-                start=(c == 0),
-                stop=(c == PASSES - 1),
-            )
+        accs = {}
 
-        def store(m, accs, second_engine_copy):
-            result = results.tile([P, FEATURES], F32)
-            nc.scalar.copy(out=result[:, 0:N_TILE], in_=accs[0][:])
-            second_engine_copy(out=result[:, N_TILE : 2 * N_TILE], in_=accs[1][:])
+        def multiply(m, c):
+            for n in range(N_TILES):
+                if c == 0:
+                    accs[(m, n)] = psum.tile([P, N_TILE], F32, name="acc")
+                m_cols = slice(m * M_TILE, (m + 1) * M_TILE)
+                n_cols = slice(n * N_TILE, (n + 1) * N_TILE)
+                nc.tensor.matmul_mx(
+                    out=accs[(m, n)][:],
+                    lhsT=da_codes[:, c, m_cols].bitcast(E5M2_X4),
+                    lhsT_scale=da_scales[:, c, m_cols],
+                    rhs=z_codes[:, c, n_cols].bitcast(E4M3_X4),
+                    rhs_scale=z_scales[:, c, n_cols],
+                    start=(c == 0),
+                    stop=(c == PASSES - 1),
+                )
+
+        def store(m, copies):
+            result = results.tile([P, FEATURES], F32, name="result")
+            for n in range(N_TILES):
+                copies[n](out=result[:, n * N_TILE : (n + 1) * N_TILE], in_=accs[(m, n)][:])
             nc.sync.dma_start(out=out[m * M_TILE : (m + 1) * M_TILE, :], in_=result[:])
 
+        on_scalar = [nc.scalar.copy, nc.scalar.copy]
+        on_both = [nc.scalar.copy, nc.vector.tensor_copy]
+
         with tc.manual_schedule():
-            load_da_inputs(0)
-            load_z_inputs(0)
-            load_z_inputs(1)
-            load_da_inputs(1)
+
+            for rows in halves:
+                load_cell(0, rows)
+                load_gh(0, rows)
+                load_o(0, rows)
+                load_gc(0, rows)
+            load_f(0)
+            load_cell(1, halves[0])
+            load_z(0)
+            load_gh(1, halves[0])
+            load_o(1, halves[0])
+            load_gc(1, halves[0])
+            load_cell(1, halves[1])
+            load_z(1)
+            load_gh(1, halves[1])
+            load_o(1, halves[1])
+            load_gc(1, halves[1])
+            load_f_half(1, 0)
+            load_f_half(1, 1)
 
             for rows in halves:
                 tanh_squared(0, rows)
-                minus_dc(0, rows)
-            for k in range(F_CHUNKS):
-                centred_f_squared(0, k)
-            form_and_quantise_da(0, range(0, 2), WIDE_DA_COLS)
-            add_z(0)
-            form_and_quantise_da(0, range(2, 4), WIDE_DA_COLS)
-            add_z(1)
-            for k in range(Z_CHUNKS):
-                regroup_z(0, k)
-            for k in range(Z_CHUNKS):
-                quantise_z(0, k)
-
-            early = {}
-            for m in range(EARLY_M_TILES):
-                for n in range(N_TILES):
-                    early[(m, n)] = psum.tile([P, N_TILE], F32, name="acc")
-                    multiply(early[(m, n)], m, n, 0)
-
+                times_gh(0, rows)
+                times_tanh(0, rows)
+                minus_dc_rows(0, rows)
+            for k in range(DA_CHUNKS):
+                f_squared_rows(0, k)
+            form_da_rows(0, 0)
+            form_da_rows(0, 1)
+            quantise_da(0, 0)
+            form_da_rows(0, 2)
+            quantise_da(0, 1)
+            form_da_rows(0, 3)
+            quantise_da(0, 2)
+            add_zk(0, 0)
+            quantise_da(0, 3)
+            add_zk(0, 1)
             tanh_squared(1, halves[0])
             for k in range(Z_CHUNKS):
-                regroup_z(1, k)
+                regroup_z(0, k)
+            times_gh(1, halves[0])
+            times_tanh(1, halves[0])
             tanh_squared(1, halves[1])
-            minus_dc(1, halves[0])
-            for k in range(Z_CHUNKS):
-                quantise_z(1, k)
-            minus_dc(1, halves[1])
-            for k in range(F_CHUNKS):
-                centred_f_squared(1, k)
-            form_and_quantise_da(1, range(DA_CHUNKS), DA_COLS)
-
-            for m in range(EARLY_M_TILES):
-                for n in range(N_TILES):
-                    multiply(early[(m, n)], m, n, 1)
-                store(m, [early[(m, n)] for n in range(N_TILES)], nc.scalar.copy)
-
-            for m in range(EARLY_M_TILES, M_TILES):
-                accs = []
-                for n in range(N_TILES):
-                    acc = psum.tile([P, N_TILE], F32, name="acc")
-                    for c in range(PASSES):
-                        multiply(acc, m, n, c)
-                    accs.append(acc)
-                store(m, accs, nc.vector.tensor_copy)
+            quantise_z(0, 0)
+            minus_dc_rows(1, halves[0])
+            quantise_z(0, 1)
+            for m in range(4):
+                multiply(m, 0)
+            add_zk(1, 0)
+            add_zk(1, 1)
+            regroup_z(1, 0)
+            regroup_z(1, 1)
+            times_gh_half(1, halves[1], 0)
+            times_tanh_half(1, halves[1], 0)
+            f_squared_rows(1, 0)
+            f_squared_rows(1, 1)
+            f_squared_rows(1, 2)
+            f_squared_rows(1, 3)
+            quantise_z(1, 0)
+            minus_dc_half(1, halves[1], 0)
+            quantise_z(1, 1)
+            form_m(1, 0)
+            form_m(1, 1)
+            quant_m(1, 0)
+            multiply(0, 1)
+            times_gh_half(1, halves[1], 1)
+            quant_m(1, 1)
+            multiply(1, 1)
+            store(0, on_scalar)
+            form_m(1, 2)
+            times_tanh_half(1, halves[1], 1)
+            quant_m(1, 2)
+            multiply(2, 1)
+            multiply(4, 0)
+            store(1, on_scalar)
+            form_m(1, 3)
+            minus_dc_half(1, halves[1], 1)
+            multiply(5, 0)
+            quant_m(1, 3)
+            multiply(3, 1)
+            store(2, on_scalar)
+            multiply(6, 0)
+            form_m(1, 4)
+            form_m(1, 5)
+            quant_m(1, 4)
+            multiply(4, 1)
+            store(3, on_scalar)
+            form_m(1, 6)
+            quant_m(1, 5)
+            multiply(5, 1)
+            multiply(7, 0)
+            store(4, on_scalar)
+            form_m(1, 7)
+            quant_m(1, 6)
+            multiply(6, 1)
+            quant_m(1, 7)
+            multiply(7, 1)
+            store(5, on_scalar)
+            store(6, [nc.vector.tensor_copy, nc.vector.tensor_copy])
+            store(7, on_both)

@@ -1,4 +1,5 @@
 import concourse.mybir as mybir
+from concourse.masks import make_identity
 
 F32 = mybir.dt.float32
 BF16 = mybir.dt.bfloat16
@@ -78,6 +79,9 @@ def tile_lstmcell_pa_v_kernel(
         x_t = pass_tiles("x", BF16)
         h_t = pass_tiles("h", BF16)
 
+
+        ident = resident.tile([P, P], BF16, name="ident")
+        make_identity(nc, ident[:])
 
         da_codes = resident.tile([P, PASSES, FEATURES], U32, align_bytes=64)
         da_scales = resident.tile([P, PASSES, FEATURES], U8, align_bytes=64)
@@ -168,20 +172,20 @@ def tile_lstmcell_pa_v_kernel(
                 out=o, in0=cell_t[c][:, js, u * 512 : (u + 1) * 512], scalar=1.0, in1=o, op0=ALU.subtract, op1=ALU.mult
             )
 
-        def form_m(c, m):
-            cols = slice(m * M_TILE, (m + 1) * M_TILE)
-            da_g[(c, m)] = grouped.tile([P, M_TILE, PACK], BF16, align_bytes=64, name="da_g")
+        def form_m(c, m, n=1):
+            cols = slice(m * M_TILE, (m + n) * M_TILE)
+            da_g[(c, m)] = grouped.tile([P, n * M_TILE, PACK], BF16, align_bytes=64, name="da_g%d" % n)
             nc.vector.scalar_tensor_tensor(
                 out=da_g[(c, m)][:],
-                in0=f1_t[m // 4][:, :, (m % 4) * M_TILE : (m % 4 + 1) * M_TILE].rearrange("p j w -> p w j"),
+                in0=f1_t[m // 4][:, :, (m % 4) * M_TILE : (m % 4 + n) * M_TILE].rearrange("p j w -> p w j"),
                 scalar=0.25,
                 in1=o_t[c][:, :, cols].rearrange("p j w -> p w j"),
                 op0=ALU.subtract,
                 op1=ALU.mult,
             )
 
-        def quant_m(c, m):
-            cols = slice(m * M_TILE, (m + 1) * M_TILE)
+        def quant_m(c, m, n=1):
+            cols = slice(m * M_TILE, (m + n) * M_TILE)
             nc.vector.quantize_mx(
                 out=da_codes[:, c, cols].bitcast(E5M2_X4),
                 scales=da_scales[:, c, cols],
@@ -191,6 +195,37 @@ def tile_lstmcell_pa_v_kernel(
         def add_zk(c, k):
             x = x_t[c][:, :, z_cols(k)]
             nc.vector.tensor_tensor(out=x, in0=x, in1=h_t[c][:, :, z_cols(k)], op=ALU.add)
+
+        def form0(m, n, of=0, tot=None):
+            cols = slice(m * M_TILE, (m + n) * M_TILE)
+            tot = tot or n
+            if of == 0:
+                da_g[(0, m)] = grouped.tile([P, tot * M_TILE, PACK], BF16, align_bytes=64, name="da_gg")
+            nc.vector.scalar_tensor_tensor(
+                out=da_g[(0, m - of)][:, of * M_TILE : (of + n) * M_TILE, :],
+                in0=f_t[0][:, :, cols].rearrange("p j w -> p w j"),
+                scalar=0.25,
+                in1=o_t[0][:, :, cols].rearrange("p j w -> p w j"),
+                op0=ALU.subtract,
+                op1=ALU.mult,
+            )
+
+        def times_gh2(c, rows):
+            js = slice(rows[0], rows[-1] + 1)
+            o = o_t[c][:, js, :]
+            nc.vector.tensor_tensor(out=o, in0=o, in1=gh_t[c][:, js, :], op=ALU.mult)
+
+        def times_tanh2(c, rows):
+            js = slice(rows[0], rows[-1] + 1)
+            o = o_t[c][:, js, :]
+            nc.vector.scalar_tensor_tensor(
+                out=o, in0=cell_t[c][:, js, :], scalar=1.0, in1=o, op0=ALU.subtract, op1=ALU.mult
+            )
+
+        def minus_dc2(c, rows):
+            js = slice(rows[0], rows[-1] + 1)
+            o = o_t[c][:, js, :]
+            nc.vector.tensor_tensor(out=o, in0=o, in1=gc_t[c][:, js, :], op=ALU.subtract)
 
         def form_da_rows(c, k):
             da_grouped[(c, k)] = grouped.tile([P, DA_COLS, PACK], BF16, align_bytes=64, name="da_grouped")
@@ -217,6 +252,33 @@ def tile_lstmcell_pa_v_kernel(
                 x = x_t[c][:, :, z_cols(k)]
                 nc.vector.tensor_tensor(out=x, in0=x, in1=h_t[c][:, :, z_cols(k)], op=ALU.add)
 
+        def sum_z_bank(c, b):
+            cols = slice(b * 256, (b + 1) * 256)
+            z_bank[(c, b)] = psum.tile([P, PACK, 256], BF16, name="acc")
+            for j in all_rows:
+                nc.tensor.matmul(
+                    out=z_bank[(c, b)][:, j, :], lhsT=ident[:], rhs=x_t[c][:, j, cols], start=True, stop=False
+                )
+                nc.tensor.matmul(
+                    out=z_bank[(c, b)][:, j, :], lhsT=ident[:], rhs=h_t[c][:, j, cols], start=False, stop=True
+                )
+
+        def add_z_rest(c):
+            x = x_t[c][:, :, 768:1024]
+            nc.vector.tensor_tensor(out=x, in0=x, in1=h_t[c][:, :, 768:1024], op=ALU.add)
+
+        def regroup_quarter(c, b):
+            k = b // 2
+            if b % 2 == 0:
+                z_grouped[(c, k)] = grouped.tile([P, Z_COLS, PACK], BF16, align_bytes=64, name="z_grouped")
+            source = z_bank[(c, b)][:] if b < 3 else x_t[c][:, :, 768:1024]
+            off = (b % 2) * 256
+            nc.scalar.copy(
+                out=z_grouped[(c, k)][:, off : off + 256, :].rearrange("p (g i) j -> p g j i", i=RUN),
+                in_=source.rearrange("p j (g i) -> p g j i", i=RUN),
+            )
+
+        z_bank = {}
         z_grouped = {}
 
         def regroup_z(c, k):
@@ -257,6 +319,16 @@ def tile_lstmcell_pa_v_kernel(
                 copies[n](out=result[:, n * N_TILE : (n + 1) * N_TILE], in_=accs[(m, n)][:])
             nc.sync.dma_start(out=out[m * M_TILE : (m + 1) * M_TILE, :], in_=result[:])
 
+        result_of = {}
+
+        def copy_out(m, n, engine_copy):
+            if m not in result_of:
+                result_of[m] = results.tile([P, FEATURES], F32, name="result")
+            engine_copy(out=result_of[m][:, n * N_TILE : (n + 1) * N_TILE], in_=accs[(m, n)][:])
+
+        def store_out(m):
+            nc.sync.dma_start(out=out[m * M_TILE : (m + 1) * M_TILE, :], in_=result_of[m][:])
+
         on_scalar = [nc.scalar.copy, nc.scalar.copy]
         on_both = [nc.scalar.copy, nc.vector.tensor_copy]
 
@@ -295,69 +367,89 @@ def tile_lstmcell_pa_v_kernel(
             quantise_da(0, 1)
             form_da_rows(0, 3)
             quantise_da(0, 2)
-            add_zk(0, 0)
             quantise_da(0, 3)
-            add_zk(0, 1)
+            add_z_rest(0)
+
             tanh_squared(1, halves[0])
-            for k in range(Z_CHUNKS):
-                regroup_z(0, k)
+            for b in range(3):
+                sum_z_bank(0, b)
+            for b in range(4):
+                regroup_quarter(0, b)
             times_gh(1, halves[0])
             times_tanh(1, halves[0])
-            tanh_squared(1, halves[1])
             quantise_z(0, 0)
             minus_dc_rows(1, halves[0])
             quantise_z(0, 1)
-            for m in range(4):
-                multiply(m, 0)
             add_zk(1, 0)
             add_zk(1, 1)
+            times_gh_half(1, halves[1], 0)
+            tanh_squared(1, halves[1])
             regroup_z(1, 0)
             regroup_z(1, 1)
-            times_gh_half(1, halves[1], 0)
-            times_tanh_half(1, halves[1], 0)
             f_squared_rows(1, 0)
             f_squared_rows(1, 1)
             f_squared_rows(1, 2)
             f_squared_rows(1, 3)
-            quantise_z(1, 0)
+            multiply(0, 0)
+            multiply(1, 0)
+            multiply(2, 0)
+            multiply(3, 0)
+            times_tanh_half(1, halves[1], 0)
             minus_dc_half(1, halves[1], 0)
+            quantise_z(1, 0)
             quantise_z(1, 1)
             form_m(1, 0)
             form_m(1, 1)
             quant_m(1, 0)
-            multiply(0, 1)
             times_gh_half(1, halves[1], 1)
             quant_m(1, 1)
-            multiply(1, 1)
-            store(0, on_scalar)
             form_m(1, 2)
             times_tanh_half(1, halves[1], 1)
             quant_m(1, 2)
-            multiply(2, 1)
-            multiply(4, 0)
-            store(1, on_scalar)
             form_m(1, 3)
             minus_dc_half(1, halves[1], 1)
-            multiply(5, 0)
             quant_m(1, 3)
-            multiply(3, 1)
-            store(2, on_scalar)
-            multiply(6, 0)
             form_m(1, 4)
             form_m(1, 5)
             quant_m(1, 4)
-            multiply(4, 1)
-            store(3, on_scalar)
             form_m(1, 6)
             quant_m(1, 5)
-            multiply(5, 1)
-            multiply(7, 0)
-            store(4, on_scalar)
             form_m(1, 7)
             quant_m(1, 6)
-            multiply(6, 1)
             quant_m(1, 7)
+            multiply(0, 1)
+            multiply(1, 1)
+            multiply(2, 1)
+            copy_out(0, 0, nc.scalar.copy)
+            copy_out(0, 1, nc.scalar.copy)
+            store_out(0)
+            copy_out(1, 0, nc.scalar.copy)
+            copy_out(1, 1, nc.scalar.copy)
+            store_out(1)
+            copy_out(2, 0, nc.scalar.copy)
+            copy_out(2, 1, nc.scalar.copy)
+            store_out(2)
+            multiply(4, 0)
+            multiply(5, 0)
+            multiply(3, 1)
+            multiply(6, 0)
+            multiply(4, 1)
+            multiply(5, 1)
+            copy_out(3, 0, nc.scalar.copy)
+            copy_out(3, 1, nc.scalar.copy)
+            store_out(3)
+            copy_out(4, 0, nc.scalar.copy)
+            copy_out(4, 1, nc.scalar.copy)
+            store_out(4)
+            copy_out(5, 0, nc.scalar.copy)
+            copy_out(5, 1, nc.scalar.copy)
+            store_out(5)
+            multiply(7, 0)
+            multiply(6, 1)
             multiply(7, 1)
-            store(5, on_scalar)
-            store(6, [nc.vector.tensor_copy, nc.vector.tensor_copy])
-            store(7, on_both)
+            copy_out(6, 0, nc.vector.tensor_copy)
+            copy_out(6, 1, nc.vector.tensor_copy)
+            store_out(6)
+            copy_out(7, 1, nc.vector.tensor_copy)
+            copy_out(7, 0, nc.scalar.copy)
+            store_out(7)

@@ -270,7 +270,7 @@ def tile_lstmcell_pa_v_kernel(
         def regroup_quarter(c, b):
             k = b // 2
             if b % 2 == 0:
-                z_grouped[(c, k)] = grouped.tile([P, Z_COLS, PACK], BF16, align_bytes=64, name="z_grouped")
+                z_grouped[(c, k)] = grouped.tile([P, Z_COLS, PACK], BF16, align_bytes=64, name="z_grouped", bufs=4)
             source = z_bank[(c, b)][:] if b < 3 else x_t[c][:, :, 768:1024]
             off = (b % 2) * 256
             nc.scalar.copy(
@@ -282,7 +282,7 @@ def tile_lstmcell_pa_v_kernel(
         z_grouped = {}
 
         def regroup_z(c, k):
-            z_grouped[(c, k)] = grouped.tile([P, Z_COLS, PACK], BF16, align_bytes=64, name="z_grouped")
+            z_grouped[(c, k)] = grouped.tile([P, Z_COLS, PACK], BF16, align_bytes=64, name="z_grouped", bufs=4)
             nc.scalar.copy(
                 out=z_grouped[(c, k)][:].rearrange("p (g i) j -> p g j i", i=RUN),
                 in_=x_t[c][:, :, z_cols(k)].rearrange("p j (g i) -> p g j i", i=RUN),
@@ -333,12 +333,14 @@ def tile_lstmcell_pa_v_kernel(
         on_both = [nc.scalar.copy, nc.vector.tensor_copy]
 
         with tc.manual_schedule():
-
-            for rows in halves:
-                load_cell(0, rows)
-                load_gh(0, rows)
-                load_o(0, rows)
-                load_gc(0, rows)
+            load_cell(0, halves[0])
+            load_gh(0, halves[0])
+            load_o(0, halves[0])
+            load_gc(0, halves[0])
+            load_cell(0, halves[1])
+            load_gh(0, halves[1])
+            load_o(0, halves[1])
+            load_gc(0, halves[1])
             load_f(0)
             load_cell(1, halves[0])
             load_z(0)
@@ -378,11 +380,12 @@ def tile_lstmcell_pa_v_kernel(
             times_gh(1, halves[0])
             times_tanh(1, halves[0])
             quantise_z(0, 0)
-            minus_dc_rows(1, halves[0])
             quantise_z(0, 1)
+            minus_dc_rows(1, halves[0])
             add_zk(1, 0)
             add_zk(1, 1)
             times_gh_half(1, halves[1], 0)
+            times_gh_half(1, halves[1], 1)
             tanh_squared(1, halves[1])
             regroup_z(1, 0)
             regroup_z(1, 1)
@@ -395,17 +398,16 @@ def tile_lstmcell_pa_v_kernel(
             multiply(2, 0)
             multiply(3, 0)
             times_tanh_half(1, halves[1], 0)
-            minus_dc_half(1, halves[1], 0)
             quantise_z(1, 0)
+            minus_dc_half(1, halves[1], 0)
             quantise_z(1, 1)
             form_m(1, 0)
             form_m(1, 1)
             quant_m(1, 0)
-            times_gh_half(1, halves[1], 1)
-            quant_m(1, 1)
             form_m(1, 2)
-            times_tanh_half(1, halves[1], 1)
+            quant_m(1, 1)
             quant_m(1, 2)
+            times_tanh_half(1, halves[1], 1)
             form_m(1, 3)
             minus_dc_half(1, halves[1], 1)
             quant_m(1, 3)
@@ -434,22 +436,22 @@ def tile_lstmcell_pa_v_kernel(
             multiply(3, 1)
             multiply(6, 0)
             multiply(4, 1)
-            multiply(5, 1)
             copy_out(3, 0, nc.scalar.copy)
             copy_out(3, 1, nc.scalar.copy)
             store_out(3)
             copy_out(4, 0, nc.scalar.copy)
             copy_out(4, 1, nc.scalar.copy)
             store_out(4)
-            copy_out(5, 0, nc.scalar.copy)
-            copy_out(5, 1, nc.scalar.copy)
-            store_out(5)
             multiply(7, 0)
+            multiply(5, 1)
             multiply(6, 1)
             multiply(7, 1)
-            copy_out(6, 0, nc.vector.tensor_copy)
+            copy_out(5, 1, nc.vector.tensor_copy)
             copy_out(6, 1, nc.vector.tensor_copy)
-            store_out(6)
             copy_out(7, 1, nc.vector.tensor_copy)
+            copy_out(5, 0, nc.scalar.copy)
+            store_out(5)
+            copy_out(6, 0, nc.scalar.copy)
+            store_out(6)
             copy_out(7, 0, nc.scalar.copy)
             store_out(7)

@@ -271,12 +271,15 @@ def tile_lstmcell_pa_v_kernel(
             k = b // 2
             if b % 2 == 0:
                 z_grouped[(c, k)] = grouped.tile([P, Z_COLS, PACK], BF16, align_bytes=64, name="z_grouped", bufs=4)
-            source = z_bank[(c, b)][:] if b < 3 else x_t[c][:, :, 768:1024]
             off = (b % 2) * 256
-            nc.scalar.copy(
-                out=z_grouped[(c, k)][:, off : off + 256, :].rearrange("p (g i) j -> p g j i", i=RUN),
-                in_=source.rearrange("p j (g i) -> p g j i", i=RUN),
-            )
+            grouped_z = z_grouped[(c, k)][:, off : off + 256, :]
+            if b < 3:
+                nc.scalar.copy(out=grouped_z, in_=z_bank[(c, b)][:].rearrange("p j w -> p w j"))
+            else:
+                nc.scalar.copy(
+                    out=grouped_z.rearrange("p (g i) j -> p g j i", i=RUN),
+                    in_=x_t[c][:, :, 768:1024].rearrange("p j (g i) -> p g j i", i=RUN),
+                )
 
         z_bank = {}
         z_grouped = {}

@@ -353,7 +353,8 @@ def tile_lstmcell_pa_v_kernel(
             load_cell(1, halves[1])
             load_z(1)
             load_gh(1, halves[1])
-            load_o(1, halves[1])
+            load_o(1, range(2, 3))
+            load_o(1, range(3, 4))
             load_gc(1, halves[1])
             load_f_half(1, 0)
             load_f_half(1, 1)
@@ -387,8 +388,7 @@ def tile_lstmcell_pa_v_kernel(
             minus_dc_rows(1, halves[0])
             add_zk(1, 0)
             add_zk(1, 1)
-            times_gh_half(1, halves[1], 0)
-            times_gh_half(1, halves[1], 1)
+            times_gh(1, halves[1])
             tanh_squared(1, halves[1])
             regroup_z(1, 0)
             regroup_z(1, 1)

@@ -254,7 +254,8 @@ def tile_lstmcell_pa_v_kernel(
 
         def sum_z_bank(c, b):
             cols = slice(b * 256, (b + 1) * 256)
-            z_bank[(c, b)] = psum.tile([P, PACK, 256], BF16, name="acc")
+            if (c, b) not in z_bank:
+                z_bank[(c, b)] = psum.tile([P, PACK, 256], BF16, name="acc")
             for j in all_rows:
                 nc.tensor.matmul(
                     out=z_bank[(c, b)][:, j, :], lhsT=ident[:], rhs=x_t[c][:, j, cols], start=True, stop=False
@@ -267,21 +268,27 @@ def tile_lstmcell_pa_v_kernel(
             x = x_t[c][:, :, 768:1024]
             nc.vector.tensor_tensor(out=x, in0=x, in1=h_t[c][:, :, 768:1024], op=ALU.add)
 
+        def add_z_second_quarter(c):
+            x = x_t[c][:, :, 256:512]
+            nc.vector.tensor_tensor(out=x, in0=x, in1=h_t[c][:, :, 256:512], op=ALU.add)
+
         def regroup_quarter(c, b):
             k = b // 2
-            if b % 2 == 0:
+            if (c, k) not in z_grouped:
                 z_grouped[(c, k)] = grouped.tile([P, Z_COLS, PACK], BF16, align_bytes=64, name="z_grouped", bufs=4)
+            source = z_bank[(c, b)][:] if (c, b) in z_bank else x_t[c][:, :, b * 256 : (b + 1) * 256]
             off = (b % 2) * 256
             grouped_z = z_grouped[(c, k)][:, off : off + 256, :]
-            if b < 3:
-                nc.scalar.copy(out=grouped_z, in_=z_bank[(c, b)][:].rearrange("p j w -> p w j"))
+            if (c, b) in z_bank:
+                nc.scalar.copy(out=grouped_z, in_=source.rearrange("p j w -> p w j"))
             else:
                 nc.scalar.copy(
                     out=grouped_z.rearrange("p (g i) j -> p g j i", i=RUN),
-                    in_=x_t[c][:, :, 768:1024].rearrange("p j (g i) -> p g j i", i=RUN),
+                    in_=source.rearrange("p j (g i) -> p g j i", i=RUN),
                 )
 
         z_bank = {}
+        z_bank[(1, 0)] = psum.tile([P, PACK, 256], BF16, name="acc")
         z_grouped = {}
 
         def regroup_z(c, k):
@@ -366,6 +373,8 @@ def tile_lstmcell_pa_v_kernel(
                 minus_dc_rows(0, rows)
             for k in range(DA_CHUNKS):
                 f_squared_rows(0, k)
+            sum_z_bank(0, 0)
+            sum_z_bank(0, 1)
             form_da_rows(0, 0)
             form_da_rows(0, 1)
             quantise_da(0, 0)
@@ -374,33 +383,34 @@ def tile_lstmcell_pa_v_kernel(
             form_da_rows(0, 3)
             quantise_da(0, 2)
             quantise_da(0, 3)
-            add_z_rest(0)
-
-            tanh_squared(1, halves[0])
-            for b in range(3):
-                sum_z_bank(0, b)
-            for b in range(4):
-                regroup_quarter(0, b)
+            add_zk(0, 1)
             times_gh(1, halves[0])
+            tanh_squared(1, halves[0])
+            regroup_z(0, 1)
+            regroup_quarter(0, 0)
+            regroup_quarter(0, 1)
+            tanh_squared(1, halves[1])
             times_tanh(1, halves[0])
             quantise_z(0, 0)
             quantise_z(0, 1)
             minus_dc_rows(1, halves[0])
-            add_zk(1, 0)
+            add_z_second_quarter(1)
             add_zk(1, 1)
-            times_gh(1, halves[1])
-            tanh_squared(1, halves[1])
-            regroup_z(1, 0)
+            times_gh(1, range(2, 3))
+            times_gh(1, range(3, 4))
+            times_tanh_half(1, halves[1], 0)
+            regroup_quarter(1, 1)
+            multiply(0, 0)
+            multiply(1, 0)
+            multiply(2, 0)
+            sum_z_bank(1, 0)
+            regroup_quarter(1, 0)
             regroup_z(1, 1)
             f_squared_rows(1, 0)
             f_squared_rows(1, 1)
             f_squared_rows(1, 2)
             f_squared_rows(1, 3)
-            multiply(0, 0)
-            multiply(1, 0)
-            multiply(2, 0)
             multiply(3, 0)
-            times_tanh_half(1, halves[1], 0)
             quantise_z(1, 0)
             minus_dc_half(1, halves[1], 0)
             quantise_z(1, 1)

@@ -16,17 +16,18 @@ K_PASS = P * PACK
 TOKENS = 1024
 FEATURES = 1024
 PASSES = TOKENS // K_PASS
-HALF_ROWS = PACK // 2
-DA_COLS = 256
-Z_COLS = 512
-RUN = 4
-DA_CHUNKS = FEATURES // DA_COLS
-Z_CHUNKS = FEATURES // Z_COLS
+HALF = FEATURES // 2
+QUARTER = FEATURES // 4
 M_TILE = 128
-N_TILE = 512
 M_TILES = FEATURES // M_TILE
-N_TILES = FEATURES // N_TILE
+HALF_TILES = M_TILES // 2
+HALVES = FEATURES // HALF
+RUN = 4
 PSUM_BANKS = 8
+EARLY_TILES = PSUM_BANKS // HALVES
+
+TENSOR_QUARTERS = [(0, 1), (0,)]
+VECTOR_COPIES = (5, 6, 7)
 
 FLOPS = 2 * TOKENS * FEATURES * FEATURES
 BYTES = TOKENS * FEATURES * (2 + 2 + 4 + 4 + 4 + 2 + 2) + FEATURES * FEATURES * 4
@@ -52,8 +53,17 @@ def tile_lstmcell_pa_v_kernel(
 ):
     nc = tc.nc
     grad_rows = grad_out.flatten_outer_dims()
-    halves = [range(u * HALF_ROWS, (u + 1) * HALF_ROWS) for u in range(PACK // HALF_ROWS)]
-    all_rows = range(PACK)
+
+    def half_cols(u):
+        return slice(u * HALF, (u + 1) * HALF)
+
+    def quarter_cols(q):
+        return slice(q * QUARTER, (q + 1) * QUARTER)
+
+    def tile_cols(m):
+        return slice(m * M_TILE, (m + 1) * M_TILE)
+
+    all_cols = slice(0, FEATURES)
 
     with (
         tc.tile_pool(name="resident", bufs=1) as resident,
@@ -69,402 +79,254 @@ def tile_lstmcell_pa_v_kernel(
 
         cell_t = pass_tiles("cell", F32)
         o_t = pass_tiles("gate_o", F32)
-        f_t = [
-            resident.tile([P, PACK, FEATURES], F32, name="gate_f0"),
-            None,
-        ]
-        f1_t = [resident.tile([P, PACK, FEATURES // 2], F32, name="gate_f1_%d" % u) for u in range(2)]
         gc_t = pass_tiles("grad_c", BF16)
         gh_t = pass_tiles("grad_h", BF16)
         x_t = pass_tiles("x", BF16)
         h_t = pass_tiles("h", BF16)
+        f_t = [
+            [resident.tile([P, PACK, FEATURES], F32, name="gate_f0")],
+            [resident.tile([P, PACK, HALF], F32, name="gate_f1_%d" % u) for u in range(HALVES)],
+        ]
 
+        z_grouped = [
+            [
+                resident.tile([P, HALF, PACK], BF16, align_bytes=64, name="z_grouped%d_%d" % (c, u))
+                for u in range(HALVES)
+            ]
+            for c in range(PASSES)
+        ]
 
-        ident = resident.tile([P, P], BF16, name="ident")
-        make_identity(nc, ident[:])
+        da_codes = resident.tile([P, PASSES, FEATURES], U32, align_bytes=64, name="da_codes")
+        da_scales = resident.tile([P, PASSES, FEATURES], U8, align_bytes=64, name="da_scales")
+        z_codes = resident.tile([P, PASSES, FEATURES], U32, align_bytes=64, name="z_codes")
+        z_scales = resident.tile([P, PASSES, FEATURES], U8, align_bytes=64, name="z_scales")
 
-        da_codes = resident.tile([P, PASSES, FEATURES], U32, align_bytes=64)
-        da_scales = resident.tile([P, PASSES, FEATURES], U8, align_bytes=64)
-        z_codes = resident.tile([P, PASSES, FEATURES], U32, align_bytes=64)
-        z_scales = resident.tile([P, PASSES, FEATURES], U8, align_bytes=64)
+        identity = resident.tile([P, P], BF16, name="identity")
+        make_identity(nc, identity[:])
 
-        def load(tile, dram, first_row, c, rows):
+        def load(tile, dram, first_row, c, rows=slice(0, PACK), cols=all_cols):
             start = first_row + c * K_PASS
             view = dram[start : start + K_PASS, :].rearrange("(p j) w -> p j w", j=PACK)
-            js = slice(rows[0], rows[-1] + 1)
-            nc.sync.dma_start(out=tile[c][:, js, :], in_=view[:, js, :])
+            nc.sync.dma_start(out=tile[:, rows, :], in_=view[:, rows, cols])
 
-        def load_cell(c, rows):
-            load(cell_t, cell, 0, c, rows)
+        row_pairs = [slice(0, 2), slice(2, 4)]
 
-        def load_gh(c, rows):
-            load(gh_t, grad_rows, TOKENS, c, rows)
-
-        def load_o(c, rows):
-            load(o_t, gate_o, 0, c, rows)
-
-        def load_gc(c, rows):
-            load(gc_t, grad_rows, 0, c, rows)
-
-        def load_f(c):
-            load(f_t, gate_f, 0, c, all_rows)
-
-        def load_f_half(c, u):
-            cols = slice(u * 512, (u + 1) * 512)
-            view = gate_f[c * K_PASS : (c + 1) * K_PASS, :].rearrange("(p j) w -> p j w", j=PACK)
-            nc.sync.dma_start(out=f1_t[u][:], in_=view[:, :, cols])
-
-        def load_z(c):
-            load(x_t, inputs, 0, c, all_rows)
-            load(h_t, short_term_memory, 0, c, all_rows)
+        def single_rows(rows):
+            return [slice(j, j + 1) for j in range(rows.start, rows.stop)]
 
         def tanh_squared(c, rows):
             for func in (ACT.Tanh, ACT.Square):
-                for j in rows:
-                    nc.scalar.activation(out=cell_t[c][:, j, :], in_=cell_t[c][:, j, :], func=func)
+                for j in single_rows(rows):
+                    t = cell_t[c][:, j, :]
+                    nc.scalar.activation(out=t, in_=t, func=func)
 
-        def times_gh(c, rows):
-            for j in rows:
-                o = o_t[c][:, j, :]
-                nc.vector.tensor_tensor(out=o, in0=o, in1=gh_t[c][:, j, :], op=ALU.mult)
+        def times_grad_h(c, rows, cols=all_cols):
+            o = o_t[c][:, rows, cols]
+            nc.vector.tensor_tensor(out=o, in0=o, in1=gh_t[c][:, rows, cols], op=ALU.mult)
 
-        def times_tanh(c, rows):
-            for j in rows:
-                o = o_t[c][:, j, :]
-                nc.vector.scalar_tensor_tensor(
-                    out=o, in0=cell_t[c][:, j, :], scalar=1.0, in1=o, op0=ALU.subtract, op1=ALU.mult
-                )
-
-        def da_cols(k):
-            return slice(k * DA_COLS, (k + 1) * DA_COLS)
-
-        def z_cols(k):
-            return slice(k * Z_COLS, (k + 1) * Z_COLS)
-
-        def f_squared_rows(c, k):
-            if c == 0:
-                f = f_t[c][:, :, da_cols(k)]
-            else:
-                f = f1_t[k // 2][:, :, da_cols(k % 2)]
-            nc.scalar.activation(out=f, in_=f, func=ACT.Square, bias=-0.5)
-
-        def minus_dc_rows(c, rows):
-            for j in rows:
-                o = o_t[c][:, j, :]
-                nc.vector.tensor_tensor(out=o, in0=o, in1=gc_t[c][:, j, :], op=ALU.subtract)
-
-        def minus_dc_half(c, rows, u):
-            js = slice(rows[0], rows[-1] + 1)
-            o = o_t[c][:, js, u * 512 : (u + 1) * 512]
-            nc.vector.tensor_tensor(out=o, in0=o, in1=gc_t[c][:, js, u * 512 : (u + 1) * 512], op=ALU.subtract)
-
-        da_g = {}
-
-        def times_gh_half(c, rows, u):
-            js = slice(rows[0], rows[-1] + 1)
-            o = o_t[c][:, js, u * 512 : (u + 1) * 512]
-            nc.vector.tensor_tensor(out=o, in0=o, in1=gh_t[c][:, js, u * 512 : (u + 1) * 512], op=ALU.mult)
-
-        def times_tanh_half(c, rows, u):
-            js = slice(rows[0], rows[-1] + 1)
-            o = o_t[c][:, js, u * 512 : (u + 1) * 512]
+        def times_tanh_term(c, rows, cols=all_cols):
+            o = o_t[c][:, rows, cols]
             nc.vector.scalar_tensor_tensor(
-                out=o, in0=cell_t[c][:, js, u * 512 : (u + 1) * 512], scalar=1.0, in1=o, op0=ALU.subtract, op1=ALU.mult
+                out=o, in0=cell_t[c][:, rows, cols], scalar=1.0, in1=o, op0=ALU.subtract, op1=ALU.mult
             )
 
-        def form_m(c, m, n=1):
-            cols = slice(m * M_TILE, (m + n) * M_TILE)
-            da_g[(c, m)] = grouped.tile([P, n * M_TILE, PACK], BF16, align_bytes=64, name="da_g%d" % n)
+        def minus_grad_c(c, rows, cols=all_cols):
+            o = o_t[c][:, rows, cols]
+            nc.vector.tensor_tensor(out=o, in0=o, in1=gc_t[c][:, rows, cols], op=ALU.subtract)
+
+        def f_view(c, cols):
+            width = FEATURES // len(f_t[c])
+            part = cols.start // width
+            return f_t[c][part][:, :, cols.start - part * width : cols.stop - part * width]
+
+        def centred_f_squared(c, q):
+            f = f_view(c, quarter_cols(q))
+            nc.scalar.activation(out=f, in_=f, func=ACT.Square, bias=-0.5)
+
+        da_grouped = {}
+
+        def form_da(c, cols):
+            da_grouped[cols.start] = grouped.tile(
+                [P, cols.stop - cols.start, PACK], BF16, align_bytes=64, name="da_grouped"
+            )
             nc.vector.scalar_tensor_tensor(
-                out=da_g[(c, m)][:],
-                in0=f1_t[m // 4][:, :, (m % 4) * M_TILE : (m % 4 + n) * M_TILE].rearrange("p j w -> p w j"),
+                out=da_grouped[cols.start][:],
+                in0=f_view(c, cols).rearrange("p j w -> p w j"),
                 scalar=0.25,
                 in1=o_t[c][:, :, cols].rearrange("p j w -> p w j"),
                 op0=ALU.subtract,
                 op1=ALU.mult,
             )
 
-        def quant_m(c, m, n=1):
-            cols = slice(m * M_TILE, (m + n) * M_TILE)
+        def quantise_da(c, cols):
             nc.vector.quantize_mx(
                 out=da_codes[:, c, cols].bitcast(E5M2_X4),
                 scales=da_scales[:, c, cols],
-                in_=da_g[(c, m)][:].rearrange("p w j -> p (w j)"),
+                in_=da_grouped[cols.start][:].rearrange("p w j -> p (w j)"),
             )
 
-        def add_zk(c, k):
-            x = x_t[c][:, :, z_cols(k)]
-            nc.vector.tensor_tensor(out=x, in0=x, in1=h_t[c][:, :, z_cols(k)], op=ALU.add)
+        def add_z(c, cols):
+            x = x_t[c][:, :, cols]
+            nc.vector.tensor_tensor(out=x, in0=x, in1=h_t[c][:, :, cols], op=ALU.add)
 
-        def form0(m, n, of=0, tot=None):
-            cols = slice(m * M_TILE, (m + n) * M_TILE)
-            tot = tot or n
-            if of == 0:
-                da_g[(0, m)] = grouped.tile([P, tot * M_TILE, PACK], BF16, align_bytes=64, name="da_gg")
-            nc.vector.scalar_tensor_tensor(
-                out=da_g[(0, m - of)][:, of * M_TILE : (of + n) * M_TILE, :],
-                in0=f_t[0][:, :, cols].rearrange("p j w -> p w j"),
-                scalar=0.25,
-                in1=o_t[0][:, :, cols].rearrange("p j w -> p w j"),
-                op0=ALU.subtract,
-                op1=ALU.mult,
-            )
+        def add_z_in_psum(c, q):
+            for j in range(PACK):
+                for summand, first in ((x_t[c], True), (h_t[c], False)):
+                    nc.tensor.matmul(
+                        out=z_banks[(c, q)][:, j, :],
+                        lhsT=identity[:],
+                        rhs=summand[:, j, quarter_cols(q)],
+                        start=first,
+                        stop=not first,
+                    )
 
-        def times_gh2(c, rows):
-            js = slice(rows[0], rows[-1] + 1)
-            o = o_t[c][:, js, :]
-            nc.vector.tensor_tensor(out=o, in0=o, in1=gh_t[c][:, js, :], op=ALU.mult)
-
-        def times_tanh2(c, rows):
-            js = slice(rows[0], rows[-1] + 1)
-            o = o_t[c][:, js, :]
-            nc.vector.scalar_tensor_tensor(
-                out=o, in0=cell_t[c][:, js, :], scalar=1.0, in1=o, op0=ALU.subtract, op1=ALU.mult
-            )
-
-        def minus_dc2(c, rows):
-            js = slice(rows[0], rows[-1] + 1)
-            o = o_t[c][:, js, :]
-            nc.vector.tensor_tensor(out=o, in0=o, in1=gc_t[c][:, js, :], op=ALU.subtract)
-
-        def form_da_rows(c, k):
-            da_grouped[(c, k)] = grouped.tile([P, DA_COLS, PACK], BF16, align_bytes=64, name="da_grouped")
-            nc.vector.scalar_tensor_tensor(
-                out=da_grouped[(c, k)][:],
-                in0=f_t[c][:, :, da_cols(k)].rearrange("p j w -> p w j"),
-                scalar=0.25,
-                in1=o_t[c][:, :, da_cols(k)].rearrange("p j w -> p w j"),
-                op0=ALU.subtract,
-                op1=ALU.mult,
-            )
-
-        da_grouped = {}
-
-        def quantise_da(c, k):
-            nc.vector.quantize_mx(
-                out=da_codes[:, c, da_cols(k)].bitcast(E5M2_X4),
-                scales=da_scales[:, c, da_cols(k)],
-                in_=da_grouped[(c, k)][:].rearrange("p w j -> p (w j)"),
-            )
-
-        def add_z(c):
-            for k in range(Z_CHUNKS):
-                x = x_t[c][:, :, z_cols(k)]
-                nc.vector.tensor_tensor(out=x, in0=x, in1=h_t[c][:, :, z_cols(k)], op=ALU.add)
-
-        def sum_z_bank(c, b):
-            cols = slice(b * 256, (b + 1) * 256)
-            if (c, b) not in z_bank:
-                z_bank[(c, b)] = psum.tile([P, PACK, 256], BF16, name="acc")
-            for j in all_rows:
-                nc.tensor.matmul(
-                    out=z_bank[(c, b)][:, j, :], lhsT=ident[:], rhs=x_t[c][:, j, cols], start=True, stop=False
-                )
-                nc.tensor.matmul(
-                    out=z_bank[(c, b)][:, j, :], lhsT=ident[:], rhs=h_t[c][:, j, cols], start=False, stop=True
-                )
-
-        def add_z_rest(c):
-            x = x_t[c][:, :, 768:1024]
-            nc.vector.tensor_tensor(out=x, in0=x, in1=h_t[c][:, :, 768:1024], op=ALU.add)
-
-        def add_z_second_quarter(c):
-            x = x_t[c][:, :, 256:512]
-            nc.vector.tensor_tensor(out=x, in0=x, in1=h_t[c][:, :, 256:512], op=ALU.add)
-
-        def regroup_quarter(c, b):
-            k = b // 2
-            if (c, k) not in z_grouped:
-                z_grouped[(c, k)] = grouped.tile([P, Z_COLS, PACK], BF16, align_bytes=64, name="z_grouped", bufs=4)
-            source = z_bank[(c, b)][:] if (c, b) in z_bank else x_t[c][:, :, b * 256 : (b + 1) * 256]
-            off = (b % 2) * 256
-            grouped_z = z_grouped[(c, k)][:, off : off + 256, :]
-            if (c, b) in z_bank:
-                nc.scalar.copy(out=grouped_z, in_=source.rearrange("p j w -> p w j"))
-            else:
-                nc.scalar.copy(
-                    out=grouped_z.rearrange("p (g i) j -> p g j i", i=RUN),
-                    in_=source.rearrange("p j (g i) -> p g j i", i=RUN),
-                )
-
-        z_bank = {}
-        z_bank[(1, 0)] = psum.tile([P, PACK, 256], BF16, name="acc")
-        z_grouped = {}
-
-        def regroup_z(c, k):
-            z_grouped[(c, k)] = grouped.tile([P, Z_COLS, PACK], BF16, align_bytes=64, name="z_grouped", bufs=4)
+        def regroup_z_from_psum(c, q):
+            u = q * QUARTER // HALF
+            first = q * QUARTER - u * HALF
             nc.scalar.copy(
-                out=z_grouped[(c, k)][:].rearrange("p (g i) j -> p g j i", i=RUN),
-                in_=x_t[c][:, :, z_cols(k)].rearrange("p j (g i) -> p g j i", i=RUN),
+                out=z_grouped[c][u][:, first : first + QUARTER, :],
+                in_=z_banks[(c, q)][:].rearrange("p j w -> p w j"),
             )
 
-        def quantise_z(c, k):
+        def regroup_z_from_sbuf(c, u, cols):
+            local = slice(cols.start - u * HALF, cols.stop - u * HALF)
+            nc.scalar.copy(
+                out=z_grouped[c][u][:, local, :].rearrange("p (g i) j -> p g j i", i=RUN),
+                in_=x_t[c][:, :, cols].rearrange("p j (g i) -> p g j i", i=RUN),
+            )
+
+        def quantise_z(c, u):
             nc.vector.quantize_mx(
-                out=z_codes[:, c, z_cols(k)].bitcast(E4M3_X4),
-                scales=z_scales[:, c, z_cols(k)],
-                in_=z_grouped[(c, k)][:].rearrange("p w j -> p (w j)"),
+                out=z_codes[:, c, half_cols(u)].bitcast(E4M3_X4),
+                scales=z_scales[:, c, half_cols(u)],
+                in_=z_grouped[c][u][:].rearrange("p w j -> p (w j)"),
             )
 
-        accs = {}
+        sums = {}
 
         def multiply(m, c):
-            for n in range(N_TILES):
+            for u in range(HALVES):
                 if c == 0:
-                    accs[(m, n)] = psum.tile([P, N_TILE], F32, name="acc")
-                m_cols = slice(m * M_TILE, (m + 1) * M_TILE)
-                n_cols = slice(n * N_TILE, (n + 1) * N_TILE)
+                    sums[(m, u)] = psum.tile([P, HALF], F32, name="bank")
                 nc.tensor.matmul_mx(
-                    out=accs[(m, n)][:],
-                    lhsT=da_codes[:, c, m_cols].bitcast(E5M2_X4),
-                    lhsT_scale=da_scales[:, c, m_cols],
-                    rhs=z_codes[:, c, n_cols].bitcast(E4M3_X4),
-                    rhs_scale=z_scales[:, c, n_cols],
+                    out=sums[(m, u)][:],
+                    lhsT=da_codes[:, c, tile_cols(m)].bitcast(E5M2_X4),
+                    lhsT_scale=da_scales[:, c, tile_cols(m)],
+                    rhs=z_codes[:, c, half_cols(u)].bitcast(E4M3_X4),
+                    rhs_scale=z_scales[:, c, half_cols(u)],
                     start=(c == 0),
                     stop=(c == PASSES - 1),
                 )
 
-        def store(m, copies):
+        def store(m):
             result = results.tile([P, FEATURES], F32, name="result")
-            for n in range(N_TILES):
-                copies[n](out=result[:, n * N_TILE : (n + 1) * N_TILE], in_=accs[(m, n)][:])
-            nc.sync.dma_start(out=out[m * M_TILE : (m + 1) * M_TILE, :], in_=result[:])
-
-        result_of = {}
-
-        def copy_out(m, n, engine_copy):
-            if m not in result_of:
-                result_of[m] = results.tile([P, FEATURES], F32, name="result")
-            engine_copy(out=result_of[m][:, n * N_TILE : (n + 1) * N_TILE], in_=accs[(m, n)][:])
-
-        def store_out(m):
-            nc.sync.dma_start(out=out[m * M_TILE : (m + 1) * M_TILE, :], in_=result_of[m][:])
-
-        on_scalar = [nc.scalar.copy, nc.scalar.copy]
-        on_both = [nc.scalar.copy, nc.vector.tensor_copy]
+            right_copy = nc.vector.tensor_copy if m in VECTOR_COPIES else nc.scalar.copy
+            nc.scalar.copy(out=result[:, half_cols(0)], in_=sums[(m, 0)][:])
+            right_copy(out=result[:, half_cols(1)], in_=sums[(m, 1)][:])
+            nc.sync.dma_start(out=out[tile_cols(m), :], in_=result[:])
 
         with tc.manual_schedule():
-            load_cell(0, halves[0])
-            load_gh(0, halves[0])
-            load_o(0, halves[0])
-            load_gc(0, halves[0])
-            load_cell(0, halves[1])
-            load_gh(0, halves[1])
-            load_o(0, halves[1])
-            load_gc(0, halves[1])
-            load_f(0)
-            load_cell(1, halves[0])
-            load_z(0)
-            load_gh(1, halves[0])
-            load_o(1, halves[0])
-            load_gc(1, halves[0])
-            load_cell(1, halves[1])
-            load_z(1)
-            load_gh(1, halves[1])
-            load_o(1, range(2, 3))
-            load_o(1, range(3, 4))
-            load_gc(1, halves[1])
-            load_f_half(1, 0)
-            load_f_half(1, 1)
+            for rows in row_pairs:
+                load(cell_t[0], cell, 0, 0, rows)
+                load(gh_t[0], grad_rows, TOKENS, 0, rows)
+                load(o_t[0], gate_o, 0, 0, rows)
+                load(gc_t[0], grad_rows, 0, 0, rows)
+            load(f_t[0][0], gate_f, 0, 0)
+            load(cell_t[1], cell, 0, 1, row_pairs[0])
+            load(x_t[0], inputs, 0, 0)
+            load(h_t[0], short_term_memory, 0, 0)
+            load(gh_t[1], grad_rows, TOKENS, 1, row_pairs[0])
+            load(o_t[1], gate_o, 0, 1, row_pairs[0])
+            load(gc_t[1], grad_rows, 0, 1, row_pairs[0])
+            load(cell_t[1], cell, 0, 1, row_pairs[1])
+            load(x_t[1], inputs, 0, 1)
+            load(h_t[1], short_term_memory, 0, 1)
+            load(gh_t[1], grad_rows, TOKENS, 1, row_pairs[1])
+            for j in single_rows(row_pairs[1]):
+                load(o_t[1], gate_o, 0, 1, j)
+            load(gc_t[1], grad_rows, 0, 1, row_pairs[1])
+            for u in range(HALVES):
+                load(f_t[1][u], gate_f, 0, 1, cols=half_cols(u))
 
-            for rows in halves:
+            for rows in row_pairs:
                 tanh_squared(0, rows)
-                times_gh(0, rows)
-                times_tanh(0, rows)
-                minus_dc_rows(0, rows)
-            for k in range(DA_CHUNKS):
-                f_squared_rows(0, k)
-            sum_z_bank(0, 0)
-            sum_z_bank(0, 1)
-            form_da_rows(0, 0)
-            form_da_rows(0, 1)
-            quantise_da(0, 0)
-            form_da_rows(0, 2)
-            quantise_da(0, 1)
-            form_da_rows(0, 3)
-            quantise_da(0, 2)
-            quantise_da(0, 3)
-            add_zk(0, 1)
-            times_gh(1, halves[0])
-            tanh_squared(1, halves[0])
-            regroup_z(0, 1)
-            regroup_quarter(0, 0)
-            regroup_quarter(0, 1)
-            tanh_squared(1, halves[1])
-            times_tanh(1, halves[0])
-            quantise_z(0, 0)
-            quantise_z(0, 1)
-            minus_dc_rows(1, halves[0])
-            add_z_second_quarter(1)
-            add_zk(1, 1)
-            times_gh(1, range(2, 3))
-            times_gh(1, range(3, 4))
-            times_tanh_half(1, halves[1], 0)
-            regroup_quarter(1, 1)
-            multiply(0, 0)
-            multiply(1, 0)
-            multiply(2, 0)
-            sum_z_bank(1, 0)
-            regroup_quarter(1, 0)
-            regroup_z(1, 1)
-            f_squared_rows(1, 0)
-            f_squared_rows(1, 1)
-            f_squared_rows(1, 2)
-            f_squared_rows(1, 3)
-            multiply(3, 0)
+                for step in (times_grad_h, times_tanh_term, minus_grad_c):
+                    for j in single_rows(rows):
+                        step(0, j)
+            for q in range(4):
+                centred_f_squared(0, q)
+            form_da(0, quarter_cols(0))
+            for q in range(1, 4):
+                form_da(0, quarter_cols(q))
+                quantise_da(0, quarter_cols(q - 1))
+            quantise_da(0, quarter_cols(3))
+
+            z_banks = {
+                (c, q): psum.tile([P, PACK, QUARTER], BF16, name="bank")
+                for c in range(PASSES)
+                for q in TENSOR_QUARTERS[c]
+            }
+            for q in TENSOR_QUARTERS[0]:
+                add_z_in_psum(0, q)
+            add_z(0, half_cols(1))
+            tanh_squared(1, row_pairs[0])
+            regroup_z_from_sbuf(0, 1, half_cols(1))
+            for q in TENSOR_QUARTERS[0]:
+                regroup_z_from_psum(0, q)
+            tanh_squared(1, row_pairs[1])
+
+            for step in (times_grad_h, times_tanh_term):
+                for j in single_rows(row_pairs[0]):
+                    step(1, j)
+            for u in range(HALVES):
+                quantise_z(0, u)
+            for j in single_rows(row_pairs[0]):
+                minus_grad_c(1, j)
+
+            for m in range(EARLY_TILES - 1):
+                multiply(m, 0)
+
+            add_z(1, quarter_cols(1))
+            add_z(1, half_cols(1))
+            for q in TENSOR_QUARTERS[1]:
+                add_z_in_psum(1, q)
+            regroup_z_from_sbuf(1, 0, quarter_cols(1))
+            for q in TENSOR_QUARTERS[1]:
+                regroup_z_from_psum(1, q)
+            regroup_z_from_sbuf(1, 1, half_cols(1))
+            multiply(EARLY_TILES - 1, 0)
+
+            for j in single_rows(row_pairs[1]):
+                times_grad_h(1, j)
+            times_tanh_term(1, row_pairs[1], half_cols(0))
             quantise_z(1, 0)
-            minus_dc_half(1, halves[1], 0)
+            minus_grad_c(1, row_pairs[1], half_cols(0))
             quantise_z(1, 1)
-            form_m(1, 0)
-            form_m(1, 1)
-            quant_m(1, 0)
-            form_m(1, 2)
-            quant_m(1, 1)
-            quant_m(1, 2)
-            times_tanh_half(1, halves[1], 1)
-            form_m(1, 3)
-            minus_dc_half(1, halves[1], 1)
-            quant_m(1, 3)
-            form_m(1, 4)
-            form_m(1, 5)
-            quant_m(1, 4)
-            form_m(1, 6)
-            quant_m(1, 5)
-            form_m(1, 7)
-            quant_m(1, 6)
-            quant_m(1, 7)
-            multiply(0, 1)
-            multiply(1, 1)
-            multiply(2, 1)
-            copy_out(0, 0, nc.scalar.copy)
-            copy_out(0, 1, nc.scalar.copy)
-            store_out(0)
-            copy_out(1, 0, nc.scalar.copy)
-            copy_out(1, 1, nc.scalar.copy)
-            store_out(1)
-            copy_out(2, 0, nc.scalar.copy)
-            copy_out(2, 1, nc.scalar.copy)
-            store_out(2)
-            multiply(4, 0)
-            multiply(5, 0)
-            multiply(3, 1)
-            multiply(6, 0)
-            multiply(4, 1)
-            copy_out(3, 0, nc.scalar.copy)
-            copy_out(3, 1, nc.scalar.copy)
-            store_out(3)
-            copy_out(4, 0, nc.scalar.copy)
-            copy_out(4, 1, nc.scalar.copy)
-            store_out(4)
-            multiply(7, 0)
-            multiply(5, 1)
-            multiply(6, 1)
-            multiply(7, 1)
-            copy_out(5, 1, nc.vector.tensor_copy)
-            copy_out(6, 1, nc.vector.tensor_copy)
-            copy_out(7, 1, nc.vector.tensor_copy)
-            copy_out(5, 0, nc.scalar.copy)
-            store_out(5)
-            copy_out(6, 0, nc.scalar.copy)
-            store_out(6)
-            copy_out(7, 0, nc.scalar.copy)
-            store_out(7)
+            for q in range(4):
+                centred_f_squared(1, q)
+
+            form_da(1, tile_cols(0))
+            for m in range(1, HALF_TILES):
+                if m == HALF_TILES - 1:
+                    times_tanh_term(1, row_pairs[1], half_cols(1))
+                form_da(1, tile_cols(m))
+                quantise_da(1, tile_cols(m - 1))
+            minus_grad_c(1, row_pairs[1], half_cols(1))
+            quantise_da(1, tile_cols(HALF_TILES - 1))
+
+            def finish(m):
+                multiply(m, 1)
+                if EARLY_TILES <= m + EARLY_TILES - 1 < M_TILES:
+                    multiply(m + EARLY_TILES - 1, 0)
+                store(m)
+
+            for m in range(HALF_TILES):
+                finish(m)
+
+            form_da(1, tile_cols(HALF_TILES))
+            for m in range(HALF_TILES + 1, M_TILES):
+                form_da(1, tile_cols(m))
+                quantise_da(1, tile_cols(m - 1))
+            quantise_da(1, tile_cols(M_TILES - 1))
+            for m in range(HALF_TILES, M_TILES):
+                finish(m)

import concourse.mybir as mybir
from concourse.masks import make_identity

F32 = mybir.dt.float32
BF16 = mybir.dt.bfloat16
U32 = mybir.dt.uint32
U8 = mybir.dt.uint8
E4M3_X4 = mybir.dt.float8_e4m3fn_x4
E5M2_X4 = mybir.dt.float8_e5m2_x4
ACT = mybir.ActivationFunctionType
ALU = mybir.AluOpType

P = 128
PACK = 4
K_PASS = P * PACK
TOKENS = 1024
FEATURES = 1024
PASSES = TOKENS // K_PASS
HALF = FEATURES // 2
QUARTER = FEATURES // 4
M_TILE = 128
M_TILES = FEATURES // M_TILE
HALF_TILES = M_TILES // 2
HALVES = FEATURES // HALF
RUN = 4
PSUM_BANKS = 8
EARLY_TILES = PSUM_BANKS // HALVES

TENSOR_QUARTERS = [(0, 1), (0,)]
VECTOR_COPIES = (5, 6, 7)

FLOPS = 2 * TOKENS * FEATURES * FEATURES
BYTES = TOKENS * FEATURES * (2 + 2 + 4 + 4 + 4 + 2 + 2) + FEATURES * FEATURES * 4


def tile_lstmcell_pa_v_kernel(
    tc,
    inputs,
    short_term_memory,
    Wf,
    b_f,
    Wi,
    b_i,
    Wg,
    b_g,
    Wo,
    b_o,
    gate_f,
    gate_o,
    cell,
    grad_out,
    out,
):
    nc = tc.nc
    grad_rows = grad_out.flatten_outer_dims()

    def half_cols(u):
        return slice(u * HALF, (u + 1) * HALF)

    def quarter_cols(q):
        return slice(q * QUARTER, (q + 1) * QUARTER)

    def tile_cols(m):
        return slice(m * M_TILE, (m + 1) * M_TILE)

    all_cols = slice(0, FEATURES)

    with (
        tc.tile_pool(name="resident", bufs=1) as resident,
        tc.tile_pool(name="grouped", bufs=3) as grouped,
        tc.tile_pool(name="results", bufs=6) as results,
        tc.psum_pool(name="psum", bufs=PSUM_BANKS) as psum,
    ):
        def pass_tiles(name, dtype):
            return [
                resident.tile([P, PACK, FEATURES], dtype, name="%s%d" % (name, c))
                for c in range(PASSES)
            ]

        cell_t = pass_tiles("cell", F32)
        o_t = pass_tiles("gate_o", F32)
        gc_t = pass_tiles("grad_c", BF16)
        gh_t = pass_tiles("grad_h", BF16)
        x_t = pass_tiles("x", BF16)
        h_t = pass_tiles("h", BF16)
        f_t = [
            [resident.tile([P, PACK, FEATURES], F32, name="gate_f0")],
            [resident.tile([P, PACK, HALF], F32, name="gate_f1_%d" % u) for u in range(HALVES)],
        ]

        z_grouped = [
            [
                resident.tile([P, HALF, PACK], BF16, align_bytes=64, name="z_grouped%d_%d" % (c, u))
                for u in range(HALVES)
            ]
            for c in range(PASSES)
        ]

        da_codes = resident.tile([P, PASSES, FEATURES], U32, align_bytes=64, name="da_codes")
        da_scales = resident.tile([P, PASSES, FEATURES], U8, align_bytes=64, name="da_scales")
        z_codes = resident.tile([P, PASSES, FEATURES], U32, align_bytes=64, name="z_codes")
        z_scales = resident.tile([P, PASSES, FEATURES], U8, align_bytes=64, name="z_scales")

        identity = resident.tile([P, P], BF16, name="identity")
        make_identity(nc, identity[:])

        def load(tile, dram, first_row, c, rows=slice(0, PACK), cols=all_cols):
            start = first_row + c * K_PASS
            view = dram[start : start + K_PASS, :].rearrange("(p j) w -> p j w", j=PACK)
            nc.sync.dma_start(out=tile[:, rows, :], in_=view[:, rows, cols])

        row_pairs = [slice(0, 2), slice(2, 4)]

        def single_rows(rows):
            return [slice(j, j + 1) for j in range(rows.start, rows.stop)]

        def tanh_squared(c, rows):
            for func in (ACT.Tanh, ACT.Square):
                for j in single_rows(rows):
                    t = cell_t[c][:, j, :]
                    nc.scalar.activation(out=t, in_=t, func=func)

        def times_grad_h(c, rows, cols=all_cols):
            o = o_t[c][:, rows, cols]
            nc.vector.tensor_tensor(out=o, in0=o, in1=gh_t[c][:, rows, cols], op=ALU.mult)

        def times_tanh_term(c, rows, cols=all_cols):
            o = o_t[c][:, rows, cols]
            nc.vector.scalar_tensor_tensor(
                out=o, in0=cell_t[c][:, rows, cols], scalar=1.0, in1=o, op0=ALU.subtract, op1=ALU.mult
            )

        def minus_grad_c(c, rows, cols=all_cols):
            o = o_t[c][:, rows, cols]
            nc.vector.tensor_tensor(out=o, in0=o, in1=gc_t[c][:, rows, cols], op=ALU.subtract)

        def f_view(c, cols):
            width = FEATURES // len(f_t[c])
            part = cols.start // width
            return f_t[c][part][:, :, cols.start - part * width : cols.stop - part * width]

        def centred_f_squared(c, q):
            f = f_view(c, quarter_cols(q))
            nc.scalar.activation(out=f, in_=f, func=ACT.Square, bias=-0.5)

        da_grouped = {}

        def form_da(c, cols):
            da_grouped[cols.start] = grouped.tile(
                [P, cols.stop - cols.start, PACK], BF16, align_bytes=64, name="da_grouped"
            )
            nc.vector.scalar_tensor_tensor(
                out=da_grouped[cols.start][:],
                in0=f_view(c, cols).rearrange("p j w -> p w j"),
                scalar=0.25,
                in1=o_t[c][:, :, cols].rearrange("p j w -> p w j"),
                op0=ALU.subtract,
                op1=ALU.mult,
            )

        def quantise_da(c, cols):
            nc.vector.quantize_mx(
                out=da_codes[:, c, cols].bitcast(E5M2_X4),
                scales=da_scales[:, c, cols],
                in_=da_grouped[cols.start][:].rearrange("p w j -> p (w j)"),
            )

        def add_z(c, cols):
            x = x_t[c][:, :, cols]
            nc.vector.tensor_tensor(out=x, in0=x, in1=h_t[c][:, :, cols], op=ALU.add)

        def add_z_in_psum(c, q):
            for j in range(PACK):
                for summand, first in ((x_t[c], True), (h_t[c], False)):
                    nc.tensor.matmul(
                        out=z_banks[(c, q)][:, j, :],
                        lhsT=identity[:],
                        rhs=summand[:, j, quarter_cols(q)],
                        start=first,
                        stop=not first,
                    )

        def regroup_z_from_psum(c, q):
            u = q * QUARTER // HALF
            first = q * QUARTER - u * HALF
            nc.scalar.copy(
                out=z_grouped[c][u][:, first : first + QUARTER, :],
                in_=z_banks[(c, q)][:].rearrange("p j w -> p w j"),
            )

        def regroup_z_from_sbuf(c, u, cols):
            local = slice(cols.start - u * HALF, cols.stop - u * HALF)
            nc.scalar.copy(
                out=z_grouped[c][u][:, local, :].rearrange("p (g i) j -> p g j i", i=RUN),
                in_=x_t[c][:, :, cols].rearrange("p j (g i) -> p g j i", i=RUN),
            )

        def quantise_z(c, u):
            nc.vector.quantize_mx(
                out=z_codes[:, c, half_cols(u)].bitcast(E4M3_X4),
                scales=z_scales[:, c, half_cols(u)],
                in_=z_grouped[c][u][:].rearrange("p w j -> p (w j)"),
            )

        sums = {}

        def multiply(m, c):
            for u in range(HALVES):
                if c == 0:
                    sums[(m, u)] = psum.tile([P, HALF], F32, name="bank")
                nc.tensor.matmul_mx(
                    out=sums[(m, u)][:],
                    lhsT=da_codes[:, c, tile_cols(m)].bitcast(E5M2_X4),
                    lhsT_scale=da_scales[:, c, tile_cols(m)],
                    rhs=z_codes[:, c, half_cols(u)].bitcast(E4M3_X4),
                    rhs_scale=z_scales[:, c, half_cols(u)],
                    start=(c == 0),
                    stop=(c == PASSES - 1),
                )

        def store(m):
            result = results.tile([P, FEATURES], F32, name="result")
            right_copy = nc.vector.tensor_copy if m in VECTOR_COPIES else nc.scalar.copy
            nc.scalar.copy(out=result[:, half_cols(0)], in_=sums[(m, 0)][:])
            right_copy(out=result[:, half_cols(1)], in_=sums[(m, 1)][:])
            nc.sync.dma_start(out=out[tile_cols(m), :], in_=result[:])

        with tc.manual_schedule():
            for rows in row_pairs:
                load(cell_t[0], cell, 0, 0, rows)
                load(gh_t[0], grad_rows, TOKENS, 0, rows)
                load(o_t[0], gate_o, 0, 0, rows)
                load(gc_t[0], grad_rows, 0, 0, rows)
            load(f_t[0][0], gate_f, 0, 0)
            load(cell_t[1], cell, 0, 1, row_pairs[0])
            load(x_t[0], inputs, 0, 0)
            load(h_t[0], short_term_memory, 0, 0)
            load(gh_t[1], grad_rows, TOKENS, 1, row_pairs[0])
            load(o_t[1], gate_o, 0, 1, row_pairs[0])
            load(gc_t[1], grad_rows, 0, 1, row_pairs[0])
            load(cell_t[1], cell, 0, 1, row_pairs[1])
            load(x_t[1], inputs, 0, 1)
            load(h_t[1], short_term_memory, 0, 1)
            load(gh_t[1], grad_rows, TOKENS, 1, row_pairs[1])
            for j in single_rows(row_pairs[1]):
                load(o_t[1], gate_o, 0, 1, j)
            load(gc_t[1], grad_rows, 0, 1, row_pairs[1])
            for u in range(HALVES):
                load(f_t[1][u], gate_f, 0, 1, cols=half_cols(u))

            for rows in row_pairs:
                tanh_squared(0, rows)
                for step in (times_grad_h, times_tanh_term, minus_grad_c):
                    for j in single_rows(rows):
                        step(0, j)
            for q in range(4):
                centred_f_squared(0, q)
            form_da(0, quarter_cols(0))
            for q in range(1, 4):
                form_da(0, quarter_cols(q))
                quantise_da(0, quarter_cols(q - 1))
            quantise_da(0, quarter_cols(3))

            z_banks = {
                (c, q): psum.tile([P, PACK, QUARTER], BF16, name="bank")
                for c in range(PASSES)
                for q in TENSOR_QUARTERS[c]
            }
            for q in TENSOR_QUARTERS[0]:
                add_z_in_psum(0, q)
            add_z(0, half_cols(1))
            tanh_squared(1, row_pairs[0])
            regroup_z_from_sbuf(0, 1, half_cols(1))
            for q in TENSOR_QUARTERS[0]:
                regroup_z_from_psum(0, q)
            tanh_squared(1, row_pairs[1])

            for step in (times_grad_h, times_tanh_term):
                for j in single_rows(row_pairs[0]):
                    step(1, j)
            for u in range(HALVES):
                quantise_z(0, u)
            for j in single_rows(row_pairs[0]):
                minus_grad_c(1, j)

            for m in range(EARLY_TILES - 1):
                multiply(m, 0)

            add_z(1, quarter_cols(1))
            add_z(1, half_cols(1))
            for q in TENSOR_QUARTERS[1]:
                add_z_in_psum(1, q)
            regroup_z_from_sbuf(1, 0, quarter_cols(1))
            for q in TENSOR_QUARTERS[1]:
                regroup_z_from_psum(1, q)
            regroup_z_from_sbuf(1, 1, half_cols(1))
            multiply(EARLY_TILES - 1, 0)

            for j in single_rows(row_pairs[1]):
                times_grad_h(1, j)
            times_tanh_term(1, row_pairs[1], half_cols(0))
            quantise_z(1, 0)
            minus_grad_c(1, row_pairs[1], half_cols(0))
            quantise_z(1, 1)
            for q in range(4):
                centred_f_squared(1, q)

            form_da(1, tile_cols(0))
            for m in range(1, HALF_TILES):
                if m == HALF_TILES - 1:
                    times_tanh_term(1, row_pairs[1], half_cols(1))
                form_da(1, tile_cols(m))
                quantise_da(1, tile_cols(m - 1))
            minus_grad_c(1, row_pairs[1], half_cols(1))
            quantise_da(1, tile_cols(HALF_TILES - 1))

            def finish(m):
                multiply(m, 1)
                if EARLY_TILES <= m + EARLY_TILES - 1 < M_TILES:
                    multiply(m + EARLY_TILES - 1, 0)
                store(m)

            for m in range(HALF_TILES):
                finish(m)

            form_da(1, tile_cols(HALF_TILES))
            for m in range(HALF_TILES + 1, M_TILES):
                form_da(1, tile_cols(m))
                quantise_da(1, tile_cols(m - 1))
            quantise_da(1, tile_cols(M_TILES - 1))
            for m in range(HALF_TILES, M_TILES):
                finish(m)
